import numpy as np
import ml_dtypes


def mxq(x, axis, fmt="e4m3"):
    dtype, down = {"e4m3": (ml_dtypes.float8_e4m3fn, 7), "e5m2": (ml_dtypes.float8_e5m2, 14)}[fmt]
    v = np.moveaxis(np.asarray(x, np.float32).astype(ml_dtypes.bfloat16).astype(np.float64), axis, -1)
    blocks = v.reshape(v.shape[:-1] + (-1, 32))
    amax = np.abs(blocks).max(-1, keepdims=True)
    byte = np.maximum(np.where(amax > 0, np.frexp(amax)[1] - 1 + 127, 0) - down, 1)
    scale = np.exp2(byte - 127.0)
    codes = (blocks / scale).astype(np.float32).astype(dtype).astype(np.float64)
    return np.moveaxis((codes * scale).reshape(v.shape), -1, axis)


WIDE = False


def mx_kscale(k):
    if not WIDE:
        return np.ones(k)
    levels = np.array([10, -10, 5, -5, 0])
    a = np.random.permutation(np.resize(levels, k // 512 * 4)).reshape(k // 512, 4)
    idx = np.arange(k)
    return np.exp2(a[idx // 512, idx % 128 // 32])


BF16 = ml_dtypes.bfloat16


def bf(x):
    return np.asarray(x, np.float32).astype(BF16)


def f64(x):
    return np.asarray(x).astype(np.float64)


E2M1 = np.array([0.0, 0.5, 1.0, 1.5, 2.0, 3.0, 4.0, 6.0, -0.0, -0.5, -1.0, -1.5, -2.0, -3.0, -4.0, -6.0])


def pack_weight(w, fmt):
    k, n = w.shape
    w = f64(bf(w)).reshape(k // 32, 32, n)
    amax = np.abs(w).max(1)
    if fmt == "e4m3":
        byte = np.frexp(amax)[1] - 1 + 127 - 7
    else:
        mant, ex = np.frexp(amax / 6.0)
        byte = np.where(mant > 0.5, ex, ex - 1) + 127
    byte = np.clip(np.where(amax > 0, byte, 1), 1, 254)
    scaled = (w * np.exp2(127.0 - byte)[:, None, :]).reshape(k, n).astype(np.float32)
    by_word = np.ascontiguousarray(scaled.reshape(k // 512, 128, 4, n).transpose(0, 1, 3, 2))
    if fmt == "e4m3":
        words = by_word.astype(ml_dtypes.float8_e4m3fn).view(np.uint8)
    else:
        c = by_word.astype(ml_dtypes.float4_e2m1fn).view(np.uint8) & 0xF
        words = c[..., 0::2] | (c[..., 1::2] << 4)
    return np.ascontiguousarray(words), np.ascontiguousarray(byte.astype(np.uint8).reshape(k // 512, 16, n))


def unpack_weight(words, scales, fmt):
    g, p, n, _ = words.shape
    if fmt == "e4m3":
        vals = np.ascontiguousarray(words).view(ml_dtypes.float8_e4m3fn).astype(np.float64)
    else:
        nib = np.empty((g, p, n, 4), np.uint8)
        nib[..., 0::2] = words & 0xF
        nib[..., 1::2] = words >> 4
        vals = E2M1[nib]
    vals = vals * np.repeat(np.exp2(scales.astype(np.float64) - 127.0), 8, axis=1)[..., None]
    return vals.transpose(0, 1, 3, 2).reshape(g * 512, n)


B, P, WS, D, H = 2, 24, 8, 1024, 16
WN = P // WS
N = WS * WS
SHIFT = WS // 2
LN_EPS = 1e-5
FMT = "e4m3"


def layer_norm(x, g, b):
    mu = x.mean(-1, keepdims=True)
    var = x.var(-1, keepdims=True)
    return (x - mu) / np.sqrt(var + LN_EPS) * g + b


def window_merge(win):
    x = win.reshape(B, WN, WN, WS, WS, D).transpose(0, 1, 3, 2, 4, 5)
    return x.reshape(B, P, P, D)


def setup_inputs():
    s, t = mx_kscale(D), mx_kscale(D)
    x_mid = np.random.standard_normal((B, P * P, D)) * 1.4 + np.random.standard_normal((B, P * P, 1)) * 0.5
    attn_win = bf(np.random.standard_normal((B * WN * WN, N, D)) * 0.4 * s)
    x_mid = bf(x_mid)
    Wo2_words, Wo2_scales = pack_weight(np.random.standard_normal((D, D)) / np.sqrt(D) / s[:, None], FMT)
    bo2 = bf(0.1 * np.random.standard_normal(D))
    g4 = bf((1.0 + 0.1 * np.random.standard_normal(D)) * t)
    b4 = bf(0.1 * np.random.standard_normal(D) * t)
    Wl_words, Wl_scales = pack_weight(np.random.standard_normal((D, D)) / np.sqrt(D) / t[:, None], FMT)
    bl = bf(0.1 * np.random.standard_normal(D))
    return {"attn_win": attn_win,
            "x_mid": x_mid,
            "Wo2_words": Wo2_words,
            "Wo2_scales": Wo2_scales,
            "bo2": bo2,
            "g4": g4,
            "b4": b4,
            "Wl_words": Wl_words,
            "Wl_scales": Wl_scales,
            "bl": bl}


def reference(attn_win, x_mid, Wo2_words, Wo2_scales, bo2, g4, b4, Wl_words, Wl_scales, bl):
    a = (mxq(f64(attn_win), 2, "e4m3") @ unpack_weight(Wo2_words, Wo2_scales, FMT)) + f64(bo2)
    a = np.roll(window_merge(a), (-SHIFT, -SHIFT), axis=(1, 2)).reshape(B, P * P, D)
    x = f64(x_mid) + a
    h = layer_norm(x, f64(g4), f64(b4))
    return x + (mxq(h, 2, "e4m3") @ unpack_weight(Wl_words, Wl_scales, FMT)) + f64(bl)

@@ -1,0 +1,383 @@
+from contextlib import ExitStack
+
+import concourse.mybir as mybir
+from concourse.masks import make_identity
+
+FP8X4 = mybir.dt.float8_e4m3fn_x4
+BF16 = mybir.dt.bfloat16
+F32 = mybir.dt.float32
+I32 = mybir.dt.int32
+U32 = mybir.dt.uint32
+U8 = mybir.dt.uint8
+ADD = mybir.AluOpType.add
+MULT = mybir.AluOpType.mult
+ACT = mybir.ActivationFunctionType
+
+P = 128
+PACK = 4
+K_PASS = P * PACK
+D = 1024
+GROUPS = D // K_PASS
+N_BANK = 512
+HALVES = D // N_BANK
+IMAGES = 2
+SIDE = 24
+WS = 8
+SHIFT = WS // 2
+WINDOWS_PER_SIDE = SIDE // WS
+WINDOWS_PER_IMAGE = WINDOWS_PER_SIDE * WINDOWS_PER_SIDE
+PATCHES = IMAGES * SIDE * SIDE
+TILES = PATCHES // P
+WINDOWS_PER_TILE = P // (WS * WS)
+LN_EPS = 1e-5
+WO2_FIRST_ROW = 0
+WL_FIRST_ROW = PACK * GROUPS
+ATTN_AHEAD = 4
+XMID_AHEAD = 3
+
+FLOPS = 2 * 2 * PATCHES * D * D
+
+
+def rolled_runs(w):
+    if w == 0:
+        return [(0, SIDE - SHIFT, SHIFT), (SHIFT, 0, SHIFT)]
+    return [(0, WS * w - SHIFT, WS)]
+
+
+def tile_successiveswintransfomerblock_pb_kernel(
+    tc, attn_win, x_mid, Wo2_words, Wo2_scales, bo2, g4, b4, Wl_words, Wl_scales, bl, out
+):
+    nc = tc.nc
+    attn_rows = attn_win.flatten_outer_dims()
+    xmid_rows = x_mid.flatten_outer_dims()
+    out_rows = out.flatten_outer_dims()
+
+    with ExitStack() as stack:
+        stack.enter_context(tc.manual_schedule())
+        keep = stack.enter_context(tc.tile_pool(name="keep", bufs=1))
+        work = stack.enter_context(tc.tile_pool(name="work", bufs=3))
+        stats = stack.enter_context(tc.tile_pool(name="stats", bufs=4))
+        tr_psum = stack.enter_context(tc.psum_pool(name="tr_psum", bufs=4))
+        mm_psum = stack.enter_context(tc.psum_pool(name="mm_psum", bufs=4))
+
+        w_planes = keep.tile([P, D], U8, align_bytes=64)
+        wo2_w = keep.tile([P, GROUPS, D], U32, align_bytes=64)
+        wl_w = keep.tile([P, GROUPS, D], U32, align_bytes=64)
+        attn_sb = keep.tile([P, TILES, D], BF16)
+        xmid_sb = keep.tile([P, TILES, D], BF16)
+        a_grouped = keep.tile([P, GROUPS, PATCHES, PACK], BF16, align_bytes=64)
+        a_words = keep.tile([P, GROUPS, PATCHES], U32, align_bytes=64)
+        a_scales = keep.tile([P, GROUPS, PATCHES], U8, align_bytes=64)
+        x_sb = keep.tile([P, TILES, D], F32)
+        resid = keep.tile([P, TILES, D], F32)
+
+        def load_scales(scales, first_row):
+            for quad in range(4):
+                rows = slice(32 * quad + first_row, 32 * quad + first_row + PACK * GROUPS)
+                nc.sync.dma_start(
+                    out=w_planes[rows, :].bitcast(I32),
+                    in_=scales[:, 4 * quad : 4 * quad + 4, :].bitcast(I32),
+                )
+
+        def load_words(w_tile, words):
+            for g in range(GROUPS):
+                nc.sync.dma_start(
+                    out=w_tile[:, g, :].bitcast(I32),
+                    in_=words[g].rearrange("p n t -> p (n t)").bitcast(I32),
+                )
+
+        def load_rows(sb, rows, m):
+            nc.sync.dma_start(out=sb[:, m, :], in_=rows[m * P : (m + 1) * P, :])
+
+        nc.vector.memset(w_planes[:].bitcast(I32), 0)
+        load_scales(Wo2_scales, WO2_FIRST_ROW)
+        load_scales(Wl_scales, WL_FIRST_ROW)
+        for m in range(ATTN_AHEAD):
+            load_rows(attn_sb, attn_rows, m)
+        load_rows(xmid_sb, xmid_rows, 0)
+        load_words(wo2_w, Wo2_words)
+        for m in range(1, XMID_AHEAD):
+            load_rows(xmid_sb, xmid_rows, m)
+        load_words(wl_w, Wl_words)
+        for later in range(TILES - XMID_AHEAD):
+            if ATTN_AHEAD + later < TILES:
+                load_rows(attn_sb, attn_rows, ATTN_AHEAD + later)
+            load_rows(xmid_sb, xmid_rows, XMID_AHEAD + later)
+
+        gain_bf = keep.tile([P, GROUPS, PACK], BF16)
+        bias_bf = keep.tile([P, GROUPS, PACK], BF16)
+        nc.scalar.dma_start(out=gain_bf[:], in_=g4.rearrange("(g p t) -> p g t", g=GROUPS, t=PACK))
+        nc.scalar.dma_start(out=bias_bf[:], in_=b4.rearrange("(g p t) -> p g t", g=GROUPS, t=PACK))
+        bo2_all = keep.tile([P, D], BF16)
+        bl_all = keep.tile([P, D], BF16)
+        nc.scalar.dma_start(out=bo2_all[:], in_=bo2.partition_broadcast(P))
+        nc.scalar.dma_start(out=bl_all[:], in_=bl.partition_broadcast(P))
+
+        ident = keep.tile([P, P], F32)
+        make_identity(nc, ident[:])
+        eps = keep.tile([P, 1], F32)
+        nc.vector.memset(eps[:], LN_EPS)
+
+        attn_t_of = {}
+        acc_of = {}
+        neg_mean_of = {}
+        std_of = {}
+        rstd_of = {}
+        offset_of = {}
+        normed_of = {}
+        normed_t_of = {}
+        h_planes_of = {}
+        h_grouped_of = {}
+        h_words_of = {}
+        h_scales_of = {}
+
+        a_pairs = (
+            a_grouped[:]
+            .rearrange("p g n t -> p (g n t)")
+            .bitcast(F32)
+            .rearrange("p (g b r c u) -> p g b r c u", g=GROUPS, b=IMAGES, r=SIDE, c=SIDE)
+        )
+
+        def attn_transpose(m):
+            attn_pairs = attn_sb[:, m, :].bitcast(F32)
+            attn_t = tr_psum.tile([P, GROUPS, 2, P], F32, tag="tr")
+            for g in range(GROUPS):
+                for u in range(2):
+                    nc.tensor.transpose(
+                        attn_t[:, g, u, :],
+                        attn_pairs[:, 2 * P * g + u : 2 * P * (g + 1) : 2],
+                        ident[:],
+                    )
+            attn_t_of[m] = attn_t
+
+        def attn_merge_and_roll(m):
+            by_window = attn_t_of[m][:].rearrange(
+                "p g u (w i j) -> p g u w i j", w=WINDOWS_PER_TILE, i=WS, j=WS
+            )
+            copy = nc.vector.tensor_copy if m % 2 == 0 else nc.scalar.copy
+            for w in range(WINDOWS_PER_TILE):
+                window = WINDOWS_PER_TILE * m + w
+                b = window // WINDOWS_PER_IMAGE
+                wr = (window % WINDOWS_PER_IMAGE) // WINDOWS_PER_SIDE
+                wc = window % WINDOWS_PER_SIDE
+                for i0, r0, n_rows in rolled_runs(wr):
+                    for j0, c0, n_cols in rolled_runs(wc):
+                        for g in range(GROUPS):
+                            copy(
+                                out=a_pairs[:, g, b, r0 : r0 + n_rows, c0 : c0 + n_cols, :],
+                                in_=by_window[
+                                    :, g, :, w, i0 : i0 + n_rows, j0 : j0 + n_cols
+                                ].rearrange("p u i j -> p i j u"),
+                            )
+
+        def attn_quantise(m):
+            places = slice(m * P, (m + 1) * P)
+            for g in range(GROUPS):
+                nc.vector.quantize_mx(
+                    out=a_words[:, g, places].bitcast(FP8X4),
+                    scales=a_scales[:, g, places],
+                    in_=a_grouped[:, g, places, :].rearrange("p n t -> p (n t)"),
+                )
+
+        def add_bo2(m):
+            nc.gpsimd.tensor_tensor(
+                out=x_sb[:, m, :], in0=xmid_sb[:, m, :], in1=bo2_all[:], op=ADD
+            )
+
+        def product(name, m, lhs_words, lhs_scales, w_words, first_row):
+            for half in range(HALVES):
+                cols = slice(half * N_BANK, (half + 1) * N_BANK)
+                acc = mm_psum.tile([P, N_BANK], F32, tag="mm")
+                for g in range(GROUPS):
+                    nc.tensor.matmul_mx(
+                        out=acc[:],
+                        lhsT=lhs_words[g].bitcast(FP8X4),
+                        lhsT_scale=lhs_scales[g],
+                        rhs=w_words[:, g, cols].bitcast(FP8X4),
+                        rhs_scale=w_planes[first_row + PACK * g : P, cols],
+                        start=(g == 0),
+                        stop=(g == GROUPS - 1),
+                    )
+                acc_of[(name, m, half)] = acc
+
+        def project(m):
+            places = slice(m * P, (m + 1) * P)
+            product(
+                "project",
+                m,
+                [a_words[:, g, places] for g in range(GROUPS)],
+                [a_scales[:, g, places] for g in range(GROUPS)],
+                wo2_w,
+                WO2_FIRST_ROW,
+            )
+
+        def add_residual(m):
+            row_sum = stats.tile([P, HALVES], F32)
+            for half in range(HALVES):
+                cols = slice(half * N_BANK, (half + 1) * N_BANK)
+                nc.vector.scalar_tensor_tensor(
+                    out=x_sb[:, m, cols],
+                    in0=acc_of[("project", m, half)][:],
+                    scalar=1.0,
+                    in1=x_sb[:, m, cols],
+                    op0=MULT,
+                    op1=ADD,
+                    accum_out=row_sum[:, half : half + 1],
+                )
+            neg_mean = stats.tile([P, 1], F32)
+            nc.vector.tensor_scalar(
+                out=neg_mean[:],
+                in0=row_sum[:, 0:1],
+                scalar1=row_sum[:, 1:2],
+                scalar2=-1.0 / D,
+                op0=ADD,
+                op1=MULT,
+            )
+            neg_mean_of[m] = neg_mean
+
+        def add_bl(m):
+            nc.gpsimd.tensor_tensor(out=resid[:, m, :], in0=x_sb[:, m, :], in1=bl_all[:], op=ADD)
+
+        def deviation(m):
+            squares = work.tile([P, D], BF16)
+            sq_sum = stats.tile([P, 1], F32)
+            nc.scalar.activation(
+                out=squares[:],
+                in_=x_sb[:, m, :],
+                func=ACT.Square,
+                bias=neg_mean_of[m][:],
+                scale=1.0,
+                accum_out=sq_sum[:],
+            )
+            std = stats.tile([P, 1], F32)
+            nc.scalar.activation(
+                out=std[:], in_=sq_sum[:], func=ACT.Sqrt, bias=eps[:], scale=1.0 / D
+            )
+            std_of[m] = std
+
+        def invert_deviation(m):
+            rstd = stats.tile([P, 1], F32)
+            nc.vector.reciprocal(out=rstd[:], in_=std_of[m][:])
+            offset = stats.tile([P, 1], F32)
+            nc.vector.tensor_mul(out=offset[:], in0=neg_mean_of[m][:], in1=rstd[:])
+            rstd_of[m] = rstd
+            offset_of[m] = offset
+
+        def normalise(m):
+            normed = work.tile([P, D], F32)
+            nc.scalar.activation(
+                out=normed[:].rearrange("p (g t q) -> p g q t", g=GROUPS, t=PACK),
+                in_=x_sb[:, m, :].rearrange("p (g q t) -> p g q t", g=GROUPS, t=PACK),
+                func=ACT.Identity,
+                bias=offset_of[m][:],
+                scale=rstd_of[m][:],
+            )
+            normed_of[m] = normed
+
+        def normed_transpose(m):
+            for g in range(GROUPS):
+                normed_t = tr_psum.tile([P, PACK, P], F32, tag="tr")
+                for t in range(PACK):
+                    block = PACK * g + t
+                    nc.tensor.transpose(
+                        normed_t[:, t, :], normed_of[m][:, block * P : (block + 1) * P], ident[:]
+                    )
+                normed_t_of[(m, g)] = normed_t
+
+        def gain_and_bias(m):
+            h_planes = work.tile([P, GROUPS, PACK, P], BF16)
+            for g in range(GROUPS):
+                for t in range(PACK):
+                    nc.scalar.activation(
+                        out=h_planes[:, g, t, :],
+                        in_=normed_t_of[(m, g)][:, t, :],
+                        func=ACT.Identity,
+                        bias=bias[:, g, t : t + 1],
+                        scale=gain[:, g, t : t + 1],
+                    )
+            h_planes_of[m] = h_planes
+
+        def h_group(m):
+            h_grouped = work.tile([P, GROUPS, P, PACK], BF16, align_bytes=64)
+            nc.vector.tensor_copy(
+                out=h_grouped[:], in_=h_planes_of[m][:].rearrange("p g t n -> p g n t")
+            )
+            h_grouped_of[m] = h_grouped
+
+        def h_quantise(m):
+            h_words = work.tile([P, GROUPS, P], U32, align_bytes=64)
+            h_scales = work.tile([P, GROUPS, P], U8, align_bytes=64)
+            nc.vector.quantize_mx(
+                out=h_words[:].rearrange("p g n -> p (g n)").bitcast(FP8X4),
+                scales=h_scales[:].rearrange("p g n -> p (g n)"),
+                in_=h_grouped_of[m][:].rearrange("p g n t -> p (g n t)"),
+            )
+            h_words_of[m] = h_words
+            h_scales_of[m] = h_scales
+
+        def linear(m):
+            product(
+                "linear",
+                m,
+                [h_words_of[m][:, g, :] for g in range(GROUPS)],
+                [h_scales_of[m][:, g, :] for g in range(GROUPS)],
+                wl_w,
+                WL_FIRST_ROW,
+            )
+
+        def finish(m):
+            for half in range(HALVES):
+                cols = slice(half * N_BANK, (half + 1) * N_BANK)
+                nc.vector.tensor_tensor(
+                    out=resid[:, m, cols],
+                    in0=acc_of[("linear", m, half)][:],
+                    in1=resid[:, m, cols],
+                    op=ADD,
+                )
+            nc.sync.dma_start(out=out_rows[m * P : (m + 1) * P, :], in_=resid[:, m, :])
+
+        for m in range(XMID_AHEAD):
+            add_bo2(m)
+        for m in range(ATTN_AHEAD):
+            attn_transpose(m)
+            attn_merge_and_roll(m)
+        attn_quantise(0)
+        attn_quantise(1)
+        project(0)
+        gain = keep.tile([P, GROUPS, PACK], F32)
+        bias = keep.tile([P, GROUPS, PACK], F32)
+        nc.vector.tensor_copy(out=gain[:], in_=gain_bf[:])
+        nc.vector.tensor_copy(out=bias[:], in_=bias_bf[:])
+
+        for s in range(TILES + 2):
+            first, second, third = s, s - 1, s - 2
+            if 0 <= third:
+                linear(third)
+            if 0 <= second < TILES:
+                normed_transpose(second)
+            if s + ATTN_AHEAD < TILES:
+                attn_transpose(s + ATTN_AHEAD)
+            if first < TILES:
+                add_residual(first)
+                add_bl(first)
+                deviation(first)
+            if s + XMID_AHEAD < TILES:
+                add_bo2(s + XMID_AHEAD)
+            if first + 1 < TILES:
+                project(first + 1)
+            if 0 <= third:
+                finish(third)
+            if first < TILES:
+                invert_deviation(first)
+            if 0 <= second < TILES:
+                gain_and_bias(second)
+            if first < TILES:
+                normalise(first)
+            if s + ATTN_AHEAD < TILES:
+                attn_merge_and_roll(s + ATTN_AHEAD)
+            if 0 <= second < TILES:
+                h_group(second)
+            if first + 2 < TILES:
+                attn_quantise(first + 2)
+            if 0 <= second < TILES:
+                h_quantise(second)

@@ -154,7 +154,6 @@ def tile_successiveswintransfomerblock_pb_kernel(
             by_window = attn_t_of[m][:].rearrange(
                 "p g u (w i j) -> p g u w i j", w=WINDOWS_PER_TILE, i=WS, j=WS
             )
-            copy = nc.vector.tensor_copy if m % 2 == 0 else nc.scalar.copy
             for w in range(WINDOWS_PER_TILE):
                 window = WINDOWS_PER_TILE * m + w
                 b = window // WINDOWS_PER_IMAGE
@@ -163,7 +162,7 @@ def tile_successiveswintransfomerblock_pb_kernel(
                 for i0, r0, n_rows in rolled_runs(wr):
                     for j0, c0, n_cols in rolled_runs(wc):
                         for g in range(GROUPS):
-                            copy(
+                            nc.scalar.copy(
                                 out=a_pairs[:, g, b, r0 : r0 + n_rows, c0 : c0 + n_cols, :],
                                 in_=by_window[
                                     :, g, :, w, i0 : i0 + n_rows, j0 : j0 + n_cols
@@ -236,7 +235,7 @@ def tile_successiveswintransfomerblock_pb_kernel(
             neg_mean_of[m] = neg_mean
 
         def add_bl(m):
-            nc.gpsimd.tensor_tensor(out=resid[:, m, :], in0=x_sb[:, m, :], in1=bl_all[:], op=ADD)
+            nc.vector.tensor_tensor(out=resid[:, m, :], in0=x_sb[:, m, :], in1=bl_all[:], op=ADD)
 
         def deviation(m):
             squares = work.tile([P, D], BF16)
@@ -359,7 +358,6 @@ def tile_successiveswintransfomerblock_pb_kernel(
                 attn_transpose(s + ATTN_AHEAD)
             if first < TILES:
                 add_residual(first)
-                add_bl(first)
                 deviation(first)
             if s + XMID_AHEAD < TILES:
                 add_bo2(s + XMID_AHEAD)
@@ -369,6 +367,7 @@ def tile_successiveswintransfomerblock_pb_kernel(
                 finish(third)
             if first < TILES:
                 invert_deviation(first)
+                add_bl(first)
             if 0 <= second < TILES:
                 gain_and_bias(second)
             if first < TILES:

@@ -32,8 +32,8 @@ WINDOWS_PER_TILE = P // (WS * WS)
 LN_EPS = 1e-5
 WO2_FIRST_ROW = 0
 WL_FIRST_ROW = PACK * GROUPS
-ATTN_AHEAD = 4
-XMID_AHEAD = 3
+FIRST_ATTN = 3
+BL_ON_VECTOR = 3
 
 FLOPS = 2 * 2 * PATCHES * D * D
 
@@ -92,17 +92,15 @@ def tile_successiveswintransfomerblock_pb_kernel(
         nc.vector.memset(w_planes[:].bitcast(I32), 0)
         load_scales(Wo2_scales, WO2_FIRST_ROW)
         load_scales(Wl_scales, WL_FIRST_ROW)
-        for m in range(ATTN_AHEAD):
+        for m in range(FIRST_ATTN):
             load_rows(attn_sb, attn_rows, m)
-        load_rows(xmid_sb, xmid_rows, 0)
         load_words(wo2_w, Wo2_words)
-        for m in range(1, XMID_AHEAD):
+        for m in range(TILES):
             load_rows(xmid_sb, xmid_rows, m)
-        load_words(wl_w, Wl_words)
-        for later in range(TILES - XMID_AHEAD):
-            if ATTN_AHEAD + later < TILES:
-                load_rows(attn_sb, attn_rows, ATTN_AHEAD + later)
-            load_rows(xmid_sb, xmid_rows, XMID_AHEAD + later)
+            if m + FIRST_ATTN < TILES:
+                load_rows(attn_sb, attn_rows, m + FIRST_ATTN)
+            if m + 1 == FIRST_ATTN:
+                load_words(wl_w, Wl_words)
 
         gain_bf = keep.tile([P, GROUPS, PACK], BF16)
         bias_bf = keep.tile([P, GROUPS, PACK], BF16)
@@ -121,9 +119,6 @@ def tile_successiveswintransfomerblock_pb_kernel(
         attn_t_of = {}
         acc_of = {}
         neg_mean_of = {}
-        std_of = {}
-        rstd_of = {}
-        offset_of = {}
         normed_of = {}
         normed_t_of = {}
         h_planes_of = {}
@@ -235,9 +230,10 @@ def tile_successiveswintransfomerblock_pb_kernel(
             neg_mean_of[m] = neg_mean
 
         def add_bl(m):
-            nc.vector.tensor_tensor(out=resid[:, m, :], in0=x_sb[:, m, :], in1=bl_all[:], op=ADD)
+            engine = nc.vector if m < BL_ON_VECTOR else nc.gpsimd
+            engine.tensor_tensor(out=resid[:, m, :], in0=x_sb[:, m, :], in1=bl_all[:], op=ADD)
 
-        def deviation(m):
+        def normalise(m):
             squares = work.tile([P, D], BF16)
             sq_sum = stats.tile([P, 1], F32)
             nc.scalar.activation(
@@ -248,28 +244,21 @@ def tile_successiveswintransfomerblock_pb_kernel(
                 scale=1.0,
                 accum_out=sq_sum[:],
             )
-            std = stats.tile([P, 1], F32)
-            nc.scalar.activation(
-                out=std[:], in_=sq_sum[:], func=ACT.Sqrt, bias=eps[:], scale=1.0 / D
-            )
-            std_of[m] = std
-
-        def invert_deviation(m):
             rstd = stats.tile([P, 1], F32)
-            nc.vector.reciprocal(out=rstd[:], in_=std_of[m][:])
+            nc.scalar.activation(
+                out=rstd[:], in_=sq_sum[:], func=ACT.Abs_reciprocal_sqrt, bias=eps[:], scale=1.0 / D
+            )
             offset = stats.tile([P, 1], F32)
-            nc.vector.tensor_mul(out=offset[:], in0=neg_mean_of[m][:], in1=rstd[:])
-            rstd_of[m] = rstd
-            offset_of[m] = offset
-
-        def normalise(m):
+            nc.scalar.activation(
+                out=offset[:], in_=neg_mean_of[m][:], func=ACT.Identity, scale=rstd[:]
+            )
             normed = work.tile([P, D], F32)
             nc.scalar.activation(
                 out=normed[:].rearrange("p (g t q) -> p g q t", g=GROUPS, t=PACK),
                 in_=x_sb[:, m, :].rearrange("p (g q t) -> p g q t", g=GROUPS, t=PACK),
                 func=ACT.Identity,
-                bias=offset_of[m][:],
-                scale=rstd_of[m][:],
+                bias=offset[:],
+                scale=rstd[:],
             )
             normed_of[m] = normed
 
@@ -285,15 +274,23 @@ def tile_successiveswintransfomerblock_pb_kernel(
 
         def gain_and_bias(m):
             h_planes = work.tile([P, GROUPS, PACK, P], BF16)
-            for g in range(GROUPS):
-                for t in range(PACK):
-                    nc.scalar.activation(
-                        out=h_planes[:, g, t, :],
-                        in_=normed_t_of[(m, g)][:, t, :],
-                        func=ACT.Identity,
-                        bias=bias[:, g, t : t + 1],
-                        scale=gain[:, g, t : t + 1],
-                    )
+            for t in range(PACK):
+                nc.scalar.activation(
+                    out=h_planes[:, 0, t, :],
+                    in_=normed_t_of[(m, 0)][:, t, :],
+                    func=ACT.Identity,
+                    bias=bias[:, 0, t : t + 1],
+                    scale=gain[:, 0, t : t + 1],
+                )
+            for t in range(PACK):
+                nc.vector.tensor_scalar(
+                    out=h_planes[:, 1, t, :],
+                    in0=normed_t_of[(m, 1)][:, t, :],
+                    scalar1=gain[:, 1, t : t + 1],
+                    scalar2=bias[:, 1, t : t + 1],
+                    op0=MULT,
+                    op1=ADD,
+                )
             h_planes_of[m] = h_planes
 
         def h_group(m):
@@ -335,48 +332,29 @@ def tile_successiveswintransfomerblock_pb_kernel(
                 )
             nc.sync.dma_start(out=out_rows[m * P : (m + 1) * P, :], in_=resid[:, m, :])
 
-        for m in range(XMID_AHEAD):
-            add_bo2(m)
-        for m in range(ATTN_AHEAD):
-            attn_transpose(m)
-            attn_merge_and_roll(m)
-        attn_quantise(0)
-        attn_quantise(1)
-        project(0)
         gain = keep.tile([P, GROUPS, PACK], F32)
         bias = keep.tile([P, GROUPS, PACK], F32)
         nc.vector.tensor_copy(out=gain[:], in_=gain_bf[:])
         nc.vector.tensor_copy(out=bias[:], in_=bias_bf[:])
 
-        for s in range(TILES + 2):
-            first, second, third = s, s - 1, s - 2
-            if 0 <= third:
-                linear(third)
-            if 0 <= second < TILES:
-                normed_transpose(second)
-            if s + ATTN_AHEAD < TILES:
-                attn_transpose(s + ATTN_AHEAD)
-            if first < TILES:
-                add_residual(first)
-                deviation(first)
-            if s + XMID_AHEAD < TILES:
-                add_bo2(s + XMID_AHEAD)
-            if first + 1 < TILES:
-                project(first + 1)
-            if 0 <= third:
-                finish(third)
-            if first < TILES:
-                invert_deviation(first)
-                add_bl(first)
-            if 0 <= second < TILES:
-                gain_and_bias(second)
-            if first < TILES:
-                normalise(first)
-            if s + ATTN_AHEAD < TILES:
-                attn_merge_and_roll(s + ATTN_AHEAD)
-            if 0 <= second < TILES:
-                h_group(second)
-            if first + 2 < TILES:
-                attn_quantise(first + 2)
-            if 0 <= second < TILES:
-                h_quantise(second)
+        for m in range(TILES):
+            add_bo2(m)
+
+        def each(piece, m):
+            if 0 <= m < TILES:
+                piece(m)
+
+        for s in range(-5, TILES + 3):
+            each(linear, s - 3)
+            each(add_residual, s)
+            each(project, s + 1)
+            each(attn_transpose, s + 5)
+            each(add_bl, s)
+            each(gain_and_bias, s - 2)
+            each(normed_transpose, s - 1)
+            each(normalise, s)
+            each(attn_merge_and_roll, s + 5)
+            each(h_group, s - 2)
+            each(attn_quantise, s + 2)
+            each(h_quantise, s - 2)
+            each(finish, s - 3)

@@ -119,6 +119,9 @@ def tile_successiveswintransfomerblock_pb_kernel(
         attn_t_of = {}
         acc_of = {}
         neg_mean_of = {}
+        sq_sum_of = {}
+        rstd_of = {}
+        offset_of = {}
         normed_of = {}
         normed_t_of = {}
         h_planes_of = {}
@@ -233,7 +236,7 @@ def tile_successiveswintransfomerblock_pb_kernel(
             engine = nc.vector if m < BL_ON_VECTOR else nc.gpsimd
             engine.tensor_tensor(out=resid[:, m, :], in0=x_sb[:, m, :], in1=bl_all[:], op=ADD)
 
-        def normalise(m):
+        def square_sum(m):
             squares = work.tile([P, D], BF16)
             sq_sum = stats.tile([P, 1], F32)
             nc.scalar.activation(
@@ -244,21 +247,32 @@ def tile_successiveswintransfomerblock_pb_kernel(
                 scale=1.0,
                 accum_out=sq_sum[:],
             )
+            sq_sum_of[m] = sq_sum
+
+        def scale_and_offset(m):
             rstd = stats.tile([P, 1], F32)
             nc.scalar.activation(
-                out=rstd[:], in_=sq_sum[:], func=ACT.Abs_reciprocal_sqrt, bias=eps[:], scale=1.0 / D
+                out=rstd[:],
+                in_=sq_sum_of[m][:],
+                func=ACT.Abs_reciprocal_sqrt,
+                bias=eps[:],
+                scale=1.0 / D,
             )
             offset = stats.tile([P, 1], F32)
             nc.scalar.activation(
                 out=offset[:], in_=neg_mean_of[m][:], func=ACT.Identity, scale=rstd[:]
             )
+            rstd_of[m] = rstd
+            offset_of[m] = offset
+
+        def normalise(m):
             normed = work.tile([P, D], F32)
             nc.scalar.activation(
                 out=normed[:].rearrange("p (g t q) -> p g q t", g=GROUPS, t=PACK),
                 in_=x_sb[:, m, :].rearrange("p (g q t) -> p g q t", g=GROUPS, t=PACK),
                 func=ACT.Identity,
-                bias=offset[:],
-                scale=rstd[:],
+                bias=offset_of[m][:],
+                scale=rstd_of[m][:],
             )
             normed_of[m] = normed
 
@@ -272,16 +286,8 @@ def tile_successiveswintransfomerblock_pb_kernel(
                     )
                 normed_t_of[(m, g)] = normed_t
 
-        def gain_and_bias(m):
+        def gain_and_bias_on_vector(m):
             h_planes = work.tile([P, GROUPS, PACK, P], BF16)
-            for t in range(PACK):
-                nc.scalar.activation(
-                    out=h_planes[:, 0, t, :],
-                    in_=normed_t_of[(m, 0)][:, t, :],
-                    func=ACT.Identity,
-                    bias=bias[:, 0, t : t + 1],
-                    scale=gain[:, 0, t : t + 1],
-                )
             for t in range(PACK):
                 nc.vector.tensor_scalar(
                     out=h_planes[:, 1, t, :],
@@ -292,6 +298,16 @@ def tile_successiveswintransfomerblock_pb_kernel(
                     op1=ADD,
                 )
             h_planes_of[m] = h_planes
+
+        def gain_and_bias_on_scalar(m):
+            for t in range(PACK):
+                nc.scalar.activation(
+                    out=h_planes_of[m][:, 0, t, :],
+                    in_=normed_t_of[(m, 0)][:, t, :],
+                    func=ACT.Identity,
+                    bias=bias[:, 0, t : t + 1],
+                    scale=gain[:, 0, t : t + 1],
+                )
 
         def h_group(m):
             h_grouped = work.tile([P, GROUPS, P, PACK], BF16, align_bytes=64)
@@ -346,15 +362,18 @@ def tile_successiveswintransfomerblock_pb_kernel(
 
         for s in range(-5, TILES + 3):
             each(linear, s - 3)
+            each(gain_and_bias_on_vector, s - 2)
             each(add_residual, s)
             each(project, s + 1)
             each(attn_transpose, s + 5)
-            each(add_bl, s)
-            each(gain_and_bias, s - 2)
+            each(square_sum, s)
+            each(gain_and_bias_on_scalar, s - 2)
             each(normed_transpose, s - 1)
-            each(normalise, s)
+            each(scale_and_offset, s)
             each(attn_merge_and_roll, s + 5)
+            each(normalise, s)
             each(h_group, s - 2)
             each(attn_quantise, s + 2)
             each(h_quantise, s - 2)
+            each(add_bl, s)
             each(finish, s - 3)

@@ -33,7 +33,7 @@ LN_EPS = 1e-5
 WO2_FIRST_ROW = 0
 WL_FIRST_ROW = PACK * GROUPS
 FIRST_ATTN = 3
-BL_ON_VECTOR = 3
+BO2_ON_VECTOR = 4
 
 FLOPS = 2 * 2 * PATCHES * D * D
 
@@ -90,31 +90,45 @@ def tile_successiveswintransfomerblock_pb_kernel(
             nc.sync.dma_start(out=sb[:, m, :], in_=rows[m * P : (m + 1) * P, :])
 
         nc.vector.memset(w_planes[:].bitcast(I32), 0)
-        load_scales(Wo2_scales, WO2_FIRST_ROW)
-        load_scales(Wl_scales, WL_FIRST_ROW)
         for m in range(FIRST_ATTN):
             load_rows(attn_sb, attn_rows, m)
+        load_scales(Wo2_scales, WO2_FIRST_ROW)
         load_words(wo2_w, Wo2_words)
         for m in range(TILES):
             load_rows(xmid_sb, xmid_rows, m)
             if m + FIRST_ATTN < TILES:
                 load_rows(attn_sb, attn_rows, m + FIRST_ATTN)
             if m + 1 == FIRST_ATTN:
+                load_scales(Wl_scales, WL_FIRST_ROW)
                 load_words(wl_w, Wl_words)
 
         gain_bf = keep.tile([P, GROUPS, PACK], BF16)
         bias_bf = keep.tile([P, GROUPS, PACK], BF16)
         nc.scalar.dma_start(out=gain_bf[:], in_=g4.rearrange("(g p t) -> p g t", g=GROUPS, t=PACK))
         nc.scalar.dma_start(out=bias_bf[:], in_=b4.rearrange("(g p t) -> p g t", g=GROUPS, t=PACK))
-        bo2_all = keep.tile([P, D], BF16)
-        bl_all = keep.tile([P, D], BF16)
-        nc.scalar.dma_start(out=bo2_all[:], in_=bo2.partition_broadcast(P))
-        nc.scalar.dma_start(out=bl_all[:], in_=bl.partition_broadcast(P))
+        bias_rows = keep.tile([P, 2, D], BF16)
+        nc.vector.memset(bias_rows[:].rearrange("p b d -> p (b d)").bitcast(I32), 0)
+        nc.scalar.dma_start(out=bias_rows[0:1, 0, :], in_=bo2.unsqueeze(0))
+        nc.scalar.dma_start(out=bias_rows[0:1, 1, :], in_=bl.unsqueeze(0))
 
         ident = keep.tile([P, P], F32)
         make_identity(nc, ident[:])
         eps = keep.tile([P, 1], F32)
         nc.vector.memset(eps[:], LN_EPS)
+
+        ones = keep.tile([P, P], BF16)
+        nc.vector.memset(ones[:], 1.0)
+        bias_all = keep.tile([P, 2, D], BF16)
+        for which in range(2):
+            for half in range(HALVES):
+                cols = slice(half * N_BANK, (half + 1) * N_BANK)
+                spread = mm_psum.tile([P, N_BANK], F32, tag="mm")
+                nc.tensor.matmul(
+                    out=spread[:], lhsT=ones[:], rhs=bias_rows[:, which, cols], start=True, stop=True
+                )
+                nc.scalar.copy(out=bias_all[:, which, cols], in_=spread[:])
+        bo2_all = bias_all[:, 0, :]
+        bl_all = bias_all[:, 1, :]
 
         attn_t_of = {}
         acc_of = {}
@@ -177,8 +191,9 @@ def tile_successiveswintransfomerblock_pb_kernel(
                 )
 
         def add_bo2(m):
-            nc.gpsimd.tensor_tensor(
-                out=x_sb[:, m, :], in0=xmid_sb[:, m, :], in1=bo2_all[:], op=ADD
+            engine = nc.vector if m < BO2_ON_VECTOR else nc.gpsimd
+            engine.tensor_tensor(
+                out=x_sb[:, m, :], in0=xmid_sb[:, m, :], in1=bo2_all, op=ADD
             )
 
         def product(name, m, lhs_words, lhs_scales, w_words, first_row):
@@ -233,8 +248,7 @@ def tile_successiveswintransfomerblock_pb_kernel(
             neg_mean_of[m] = neg_mean
 
         def add_bl(m):
-            engine = nc.vector if m < BL_ON_VECTOR else nc.gpsimd
-            engine.tensor_tensor(out=resid[:, m, :], in0=x_sb[:, m, :], in1=bl_all[:], op=ADD)
+            nc.vector.tensor_tensor(out=resid[:, m, :], in0=x_sb[:, m, :], in1=bl_all, op=ADD)
 
         def square_sum(m):
             squares = work.tile([P, D], BF16)
@@ -286,27 +300,17 @@ def tile_successiveswintransfomerblock_pb_kernel(
                     )
                 normed_t_of[(m, g)] = normed_t
 
-        def gain_and_bias_on_vector(m):
-            h_planes = work.tile([P, GROUPS, PACK, P], BF16)
-            for t in range(PACK):
-                nc.vector.tensor_scalar(
-                    out=h_planes[:, 1, t, :],
-                    in0=normed_t_of[(m, 1)][:, t, :],
-                    scalar1=gain[:, 1, t : t + 1],
-                    scalar2=bias[:, 1, t : t + 1],
-                    op0=MULT,
-                    op1=ADD,
-                )
-            h_planes_of[m] = h_planes
-
-        def gain_and_bias_on_scalar(m):
+        def gain_and_bias(m, g):
+            if g == 0:
+                h_planes = work.tile([P, GROUPS, PACK, P], BF16)
+                h_planes_of[m] = h_planes
             for t in range(PACK):
                 nc.scalar.activation(
-                    out=h_planes_of[m][:, 0, t, :],
-                    in_=normed_t_of[(m, 0)][:, t, :],
+                    out=h_planes_of[m][:, g, t, :],
+                    in_=normed_t_of[(m, g)][:, t, :],
                     func=ACT.Identity,
-                    bias=bias[:, 0, t : t + 1],
-                    scale=gain[:, 0, t : t + 1],
+                    bias=bias[:, g, t : t + 1],
+                    scale=gain[:, g, t : t + 1],
                 )
 
         def h_group(m):
@@ -346,34 +350,32 @@ def tile_successiveswintransfomerblock_pb_kernel(
                     in1=resid[:, m, cols],
                     op=ADD,
                 )
-            nc.sync.dma_start(out=out_rows[m * P : (m + 1) * P, :], in_=resid[:, m, :])
+                nc.sync.dma_start(out=out_rows[m * P : (m + 1) * P, cols], in_=resid[:, m, cols])
 
         gain = keep.tile([P, GROUPS, PACK], F32)
         bias = keep.tile([P, GROUPS, PACK], F32)
         nc.vector.tensor_copy(out=gain[:], in_=gain_bf[:])
         nc.vector.tensor_copy(out=bias[:], in_=bias_bf[:])
 
-        for m in range(TILES):
-            add_bo2(m)
-
-        def each(piece, m):
+        def each(piece, m, *more):
             if 0 <= m < TILES:
-                piece(m)
+                piece(m, *more)
 
-        for s in range(-5, TILES + 3):
-            each(linear, s - 3)
-            each(gain_and_bias_on_vector, s - 2)
+        for s in range(-5, TILES + 4):
+            each(project, s)
             each(add_residual, s)
-            each(project, s + 1)
+            each(add_bl, s - 1)
+            each(gain_and_bias, s - 3, 0)
+            each(square_sum, s - 1)
+            each(gain_and_bias, s - 3, 1)
+            each(normed_transpose, s - 2)
             each(attn_transpose, s + 5)
-            each(square_sum, s)
-            each(gain_and_bias_on_scalar, s - 2)
-            each(normed_transpose, s - 1)
-            each(scale_and_offset, s)
-            each(attn_merge_and_roll, s + 5)
-            each(normalise, s)
-            each(h_group, s - 2)
+            each(linear, s - 4)
+            each(scale_and_offset, s - 1)
+            each(attn_merge_and_roll, s + 4)
+            each(normalise, s - 1)
+            each(h_group, s - 3)
             each(attn_quantise, s + 2)
-            each(h_quantise, s - 2)
-            each(add_bl, s)
-            each(finish, s - 3)
+            each(h_quantise, s - 3)
+            each(finish, s - 4)
+            each(add_bo2, s + 2)

@@ -248,7 +248,8 @@ def tile_successiveswintransfomerblock_pb_kernel(
             neg_mean_of[m] = neg_mean
 
         def add_bl(m):
-            nc.vector.tensor_tensor(out=resid[:, m, :], in0=x_sb[:, m, :], in1=bl_all, op=ADD)
+            engine = nc.vector if m < BO2_ON_VECTOR else nc.gpsimd
+            engine.tensor_tensor(out=resid[:, m, :], in0=x_sb[:, m, :], in1=bl_all, op=ADD)
 
         def square_sum(m):
             squares = work.tile([P, D], BF16)

@@ -173,13 +173,12 @@ def tile_successiveswintransfomerblock_pb_kernel(
                 wc = window % WINDOWS_PER_SIDE
                 for i0, r0, n_rows in rolled_runs(wr):
                     for j0, c0, n_cols in rolled_runs(wc):
-                        for g in range(GROUPS):
-                            nc.scalar.copy(
-                                out=a_pairs[:, g, b, r0 : r0 + n_rows, c0 : c0 + n_cols, :],
-                                in_=by_window[
-                                    :, g, :, w, i0 : i0 + n_rows, j0 : j0 + n_cols
-                                ].rearrange("p u i j -> p i j u"),
-                            )
+                        nc.scalar.copy(
+                            out=a_pairs[:, :, b, r0 : r0 + n_rows, c0 : c0 + n_cols, :],
+                            in_=by_window[
+                                :, :, :, w, i0 : i0 + n_rows, j0 : j0 + n_cols
+                            ].rearrange("p g u i j -> p g i j u"),
+                        )
 
         def attn_quantise(m):
             places = slice(m * P, (m + 1) * P)
@@ -248,8 +247,7 @@ def tile_successiveswintransfomerblock_pb_kernel(
             neg_mean_of[m] = neg_mean
 
         def add_bl(m):
-            engine = nc.vector if m < BO2_ON_VECTOR else nc.gpsimd
-            engine.tensor_tensor(out=resid[:, m, :], in0=x_sb[:, m, :], in1=bl_all, op=ADD)
+            nc.vector.tensor_tensor(out=resid[:, m, :], in0=x_sb[:, m, :], in1=bl_all, op=ADD)
 
         def square_sum(m):
             squares = work.tile([P, D], BF16)

@@ -30,8 +30,6 @@ PATCHES = IMAGES * SIDE * SIDE
 TILES = PATCHES // P
 WINDOWS_PER_TILE = P // (WS * WS)
 LN_EPS = 1e-5
-WO2_FIRST_ROW = 0
-WL_FIRST_ROW = PACK * GROUPS
 FIRST_ATTN = 3
 BO2_ON_VECTOR = 4
 
@@ -60,7 +58,8 @@ def tile_successiveswintransfomerblock_pb_kernel(
         tr_psum = stack.enter_context(tc.psum_pool(name="tr_psum", bufs=4))
         mm_psum = stack.enter_context(tc.psum_pool(name="mm_psum", bufs=4))
 
-        w_planes = keep.tile([P, D], U8, align_bytes=64)
+        wo2_planes = keep.tile([P, D], U8, align_bytes=64)
+        wl_planes = keep.tile([P, D], U8, align_bytes=64)
         wo2_w = keep.tile([P, GROUPS, D], U32, align_bytes=64)
         wl_w = keep.tile([P, GROUPS, D], U32, align_bytes=64)
         attn_sb = keep.tile([P, TILES, D], BF16)
@@ -71,64 +70,84 @@ def tile_successiveswintransfomerblock_pb_kernel(
         x_sb = keep.tile([P, TILES, D], F32)
         resid = keep.tile([P, TILES, D], F32)
 
-        def load_scales(scales, first_row):
+        eps = keep.tile([P, 1], F32)
+        warm = keep.tile([P, 1], F32)
+        ones = keep.tile([P, P], BF16)
+        ident = keep.tile([P, P], F32)
+        bias_rows = keep.tile([P, 2, D], BF16)
+        bias_all = keep.tile([P, 2, D], BF16)
+        gain_bf = keep.tile([P, GROUPS, PACK], BF16)
+        bias_bf = keep.tile([P, GROUPS, PACK], BF16)
+        gain = keep.tile([P, GROUPS, PACK], F32)
+        bias = keep.tile([P, GROUPS, PACK], F32)
+
+        nc.vector.memset(wo2_planes[:].bitcast(I32), 0)
+        nc.vector.memset(eps[:], LN_EPS)
+        for which in range(2):
+            nc.vector.memset(bias_rows[:, which, :].bitcast(I32), 0)
+        nc.vector.memset(ones[:], 1.0)
+        nc.vector.memset(wl_planes[:].bitcast(I32), 0)
+        make_identity(nc, ident[:])
+
+        def load_scales(planes, scales):
             for quad in range(4):
-                rows = slice(32 * quad + first_row, 32 * quad + first_row + PACK * GROUPS)
+                rows = slice(32 * quad, 32 * quad + PACK * GROUPS)
                 nc.sync.dma_start(
-                    out=w_planes[rows, :].bitcast(I32),
+                    out=planes[rows, :].bitcast(I32),
                     in_=scales[:, 4 * quad : 4 * quad + 4, :].bitcast(I32),
                 )
 
-        def load_words(w_tile, words):
-            for g in range(GROUPS):
-                nc.sync.dma_start(
-                    out=w_tile[:, g, :].bitcast(I32),
-                    in_=words[g].rearrange("p n t -> p (n t)").bitcast(I32),
-                )
+        def load_words(w_tile, words, half):
+            nc.sync.dma_start(
+                out=w_tile[:, :, half * N_BANK : (half + 1) * N_BANK].bitcast(I32),
+                in_=words.rearrange("g p n t -> p g (n t)")[
+                    :, :, PACK * half * N_BANK : PACK * (half + 1) * N_BANK
+                ].bitcast(I32),
+            )
 
         def load_rows(sb, rows, m):
             nc.sync.dma_start(out=sb[:, m, :], in_=rows[m * P : (m + 1) * P, :])
 
-        nc.vector.memset(w_planes[:].bitcast(I32), 0)
         for m in range(FIRST_ATTN):
             load_rows(attn_sb, attn_rows, m)
-        load_scales(Wo2_scales, WO2_FIRST_ROW)
-        load_words(wo2_w, Wo2_words)
-        for m in range(TILES):
+        load_rows(xmid_sb, xmid_rows, 0)
+        load_words(wo2_w, Wo2_words, 0)
+        load_scales(wo2_planes, Wo2_scales)
+        load_words(wo2_w, Wo2_words, 1)
+        for m in range(1, TILES):
+            if m + FIRST_ATTN - 1 < TILES:
+                load_rows(attn_sb, attn_rows, m + FIRST_ATTN - 1)
             load_rows(xmid_sb, xmid_rows, m)
-            if m + FIRST_ATTN < TILES:
-                load_rows(attn_sb, attn_rows, m + FIRST_ATTN)
-            if m + 1 == FIRST_ATTN:
-                load_scales(Wl_scales, WL_FIRST_ROW)
-                load_words(wl_w, Wl_words)
+            if m == FIRST_ATTN:
+                load_scales(wl_planes, Wl_scales)
+                load_words(wl_w, Wl_words, 0)
+                load_words(wl_w, Wl_words, 1)
 
-        gain_bf = keep.tile([P, GROUPS, PACK], BF16)
-        bias_bf = keep.tile([P, GROUPS, PACK], BF16)
+        nc.scalar.dma_start(out=bias_rows[0:1, 0, :], in_=bo2.unsqueeze(0))
+        nc.scalar.activation(out=warm[:], in_=eps[:], func=ACT.Identity)
+        nc.scalar.dma_start(out=bias_rows[0:1, 1, :], in_=bl.unsqueeze(0))
         nc.scalar.dma_start(out=gain_bf[:], in_=g4.rearrange("(g p t) -> p g t", g=GROUPS, t=PACK))
         nc.scalar.dma_start(out=bias_bf[:], in_=b4.rearrange("(g p t) -> p g t", g=GROUPS, t=PACK))
-        bias_rows = keep.tile([P, 2, D], BF16)
-        nc.vector.memset(bias_rows[:].rearrange("p b d -> p (b d)").bitcast(I32), 0)
-        nc.scalar.dma_start(out=bias_rows[0:1, 0, :], in_=bo2.unsqueeze(0))
-        nc.scalar.dma_start(out=bias_rows[0:1, 1, :], in_=bl.unsqueeze(0))
+        nc.gpsimd.tensor_copy(out=gain[:], in_=gain_bf[:])
+        nc.gpsimd.tensor_copy(out=bias[:], in_=bias_bf[:])
 
-        ident = keep.tile([P, P], F32)
-        make_identity(nc, ident[:])
-        eps = keep.tile([P, 1], F32)
-        nc.vector.memset(eps[:], LN_EPS)
-
-        ones = keep.tile([P, P], BF16)
-        nc.vector.memset(ones[:], 1.0)
-        bias_all = keep.tile([P, 2, D], BF16)
-        for which in range(2):
-            for half in range(HALVES):
-                cols = slice(half * N_BANK, (half + 1) * N_BANK)
-                spread = mm_psum.tile([P, N_BANK], F32, tag="mm")
-                nc.tensor.matmul(
-                    out=spread[:], lhsT=ones[:], rhs=bias_rows[:, which, cols], start=True, stop=True
-                )
-                nc.scalar.copy(out=bias_all[:, which, cols], in_=spread[:])
         bo2_all = bias_all[:, 0, :]
         bl_all = bias_all[:, 1, :]
+        spread_of = {}
+
+        def spread(which):
+            for half in range(HALVES):
+                cols = slice(half * N_BANK, (half + 1) * N_BANK)
+                spread_acc = mm_psum.tile([P, N_BANK], F32, tag="mm")
+                nc.tensor.matmul(
+                    out=spread_acc[:], lhsT=ones[:], rhs=bias_rows[:, which, cols], start=True, stop=True
+                )
+                spread_of[(which, half)] = spread_acc
+
+        def spread_copy(which):
+            for half in range(HALVES):
+                cols = slice(half * N_BANK, (half + 1) * N_BANK)
+                nc.scalar.copy(out=bias_all[:, which, cols], in_=spread_of[(which, half)][:])
 
         attn_t_of = {}
         acc_of = {}
@@ -195,7 +214,7 @@ def tile_successiveswintransfomerblock_pb_kernel(
                 out=x_sb[:, m, :], in0=xmid_sb[:, m, :], in1=bo2_all, op=ADD
             )
 
-        def product(name, m, lhs_words, lhs_scales, w_words, first_row):
+        def product(name, m, lhs_words, lhs_scales, w_words, w_planes):
             for half in range(HALVES):
                 cols = slice(half * N_BANK, (half + 1) * N_BANK)
                 acc = mm_psum.tile([P, N_BANK], F32, tag="mm")
@@ -205,7 +224,7 @@ def tile_successiveswintransfomerblock_pb_kernel(
                         lhsT=lhs_words[g].bitcast(FP8X4),
                         lhsT_scale=lhs_scales[g],
                         rhs=w_words[:, g, cols].bitcast(FP8X4),
-                        rhs_scale=w_planes[first_row + PACK * g : P, cols],
+                        rhs_scale=w_planes[PACK * g : P, cols],
                         start=(g == 0),
                         stop=(g == GROUPS - 1),
                     )
@@ -219,7 +238,7 @@ def tile_successiveswintransfomerblock_pb_kernel(
                 [a_words[:, g, places] for g in range(GROUPS)],
                 [a_scales[:, g, places] for g in range(GROUPS)],
                 wo2_w,
-                WO2_FIRST_ROW,
+                wo2_planes,
             )
 
         def add_residual(m):
@@ -337,7 +356,7 @@ def tile_successiveswintransfomerblock_pb_kernel(
                 [h_words_of[m][:, g, :] for g in range(GROUPS)],
                 [h_scales_of[m][:, g, :] for g in range(GROUPS)],
                 wl_w,
-                WL_FIRST_ROW,
+                wl_planes,
             )
 
         def finish(m):
@@ -351,16 +370,20 @@ def tile_successiveswintransfomerblock_pb_kernel(
                 )
                 nc.sync.dma_start(out=out_rows[m * P : (m + 1) * P, cols], in_=resid[:, m, cols])
 
-        gain = keep.tile([P, GROUPS, PACK], F32)
-        bias = keep.tile([P, GROUPS, PACK], F32)
-        nc.vector.tensor_copy(out=gain[:], in_=gain_bf[:])
-        nc.vector.tensor_copy(out=bias[:], in_=bias_bf[:])
-
         def each(piece, m, *more):
             if 0 <= m < TILES:
                 piece(m, *more)
 
-        for s in range(-5, TILES + 4):
+        def transpose_step(k):
+            return max(k - 5, (k - FIRST_ATTN) // 2) if k >= FIRST_ATTN else -1
+
+        def merge_step(k):
+            return max(k - 4, transpose_step(k))
+
+        def quantise_step(m):
+            return max(m - 2, merge_step(min(m + FIRST_ATTN - 1, TILES - 1)))
+
+        for s in range(-1, TILES + 4):
             each(project, s)
             each(add_residual, s)
             each(add_bl, s - 1)
@@ -368,13 +391,27 @@ def tile_successiveswintransfomerblock_pb_kernel(
             each(square_sum, s - 1)
             each(gain_and_bias, s - 3, 1)
             each(normed_transpose, s - 2)
-            each(attn_transpose, s + 5)
+            for k in range(TILES):
+                if transpose_step(k) == s:
+                    attn_transpose(k)
+            if s == -1:
+                spread(0)
+                spread(1)
             each(linear, s - 4)
             each(scale_and_offset, s - 1)
-            each(attn_merge_and_roll, s + 4)
+            for k in range(TILES):
+                if merge_step(k) == s:
+                    attn_merge_and_roll(k)
+            if s == -1:
+                spread_copy(0)
+                spread_copy(1)
             each(normalise, s - 1)
             each(h_group, s - 3)
-            each(attn_quantise, s + 2)
+            for m in range(TILES):
+                if quantise_step(m) == s:
+                    attn_quantise(m)
             each(h_quantise, s - 3)
             each(finish, s - 4)
-            each(add_bo2, s + 2)
+            for m in range(TILES):
+                if quantise_step(m) == s:
+                    add_bo2(m)

@@ -214,6 +214,9 @@ def tile_successiveswintransfomerblock_pb_kernel(
                 out=x_sb[:, m, :], in0=xmid_sb[:, m, :], in1=bo2_all, op=ADD
             )
 
+        def release_bo2(m):
+            nc.vector.memset(x_sb[:, m, 0:1], 0.0)
+
         def product(name, m, lhs_words, lhs_scales, w_words, w_planes):
             for half in range(HALVES):
                 cols = slice(half * N_BANK, (half + 1) * N_BANK)
@@ -411,7 +414,9 @@ def tile_successiveswintransfomerblock_pb_kernel(
                 if quantise_step(m) == s:
                     attn_quantise(m)
             each(h_quantise, s - 3)
-            each(finish, s - 4)
             for m in range(TILES):
                 if quantise_step(m) == s:
+                    if m >= BO2_ON_VECTOR:
+                        release_bo2(m)
                     add_bo2(m)
+            each(finish, s - 4)

@@ -31,7 +31,7 @@ TILES = PATCHES // P
 WINDOWS_PER_TILE = P // (WS * WS)
 LN_EPS = 1e-5
 FIRST_ATTN = 3
-BO2_ON_VECTOR = 4
+BO2_ON_VECTOR = 2
 
 FLOPS = 2 * 2 * PATCHES * D * D
 
@@ -114,22 +114,29 @@ def tile_successiveswintransfomerblock_pb_kernel(
         load_words(wo2_w, Wo2_words, 0)
         load_scales(wo2_planes, Wo2_scales)
         load_words(wo2_w, Wo2_words, 1)
+        nc.sync.dma_start(out=bias_rows[0:1, 1, :], in_=bl.unsqueeze(0))
         for m in range(1, TILES):
             if m + FIRST_ATTN - 1 < TILES:
                 load_rows(attn_sb, attn_rows, m + FIRST_ATTN - 1)
             load_rows(xmid_sb, xmid_rows, m)
+            if m == 1:
+                nc.sync.dma_start(
+                    out=gain_bf[:], in_=g4.rearrange("(g p t) -> p g t", g=GROUPS, t=PACK)
+                )
+                nc.sync.dma_start(
+                    out=bias_bf[:], in_=b4.rearrange("(g p t) -> p g t", g=GROUPS, t=PACK)
+                )
             if m == FIRST_ATTN:
                 load_scales(wl_planes, Wl_scales)
                 load_words(wl_w, Wl_words, 0)
                 load_words(wl_w, Wl_words, 1)
 
         nc.scalar.dma_start(out=bias_rows[0:1, 0, :], in_=bo2.unsqueeze(0))
-        nc.scalar.activation(out=warm[:], in_=eps[:], func=ACT.Identity)
-        nc.scalar.dma_start(out=bias_rows[0:1, 1, :], in_=bl.unsqueeze(0))
-        nc.scalar.dma_start(out=gain_bf[:], in_=g4.rearrange("(g p t) -> p g t", g=GROUPS, t=PACK))
-        nc.scalar.dma_start(out=bias_bf[:], in_=b4.rearrange("(g p t) -> p g t", g=GROUPS, t=PACK))
-        nc.gpsimd.tensor_copy(out=gain[:], in_=gain_bf[:])
-        nc.gpsimd.tensor_copy(out=bias[:], in_=bias_bf[:])
+        nc.scalar.activation(out=warm[:], in_=eps[:], func=ACT.Abs_reciprocal_sqrt)
+
+        def convert_gain_and_bias():
+            nc.gpsimd.tensor_copy(out=gain[:], in_=gain_bf[:])
+            nc.gpsimd.tensor_copy(out=bias[:], in_=bias_bf[:])
 
         bo2_all = bias_all[:, 0, :]
         bl_all = bias_all[:, 1, :]
@@ -258,7 +265,7 @@ def tile_successiveswintransfomerblock_pb_kernel(
                     accum_out=row_sum[:, half : half + 1],
                 )
             neg_mean = stats.tile([P, 1], F32)
-            nc.vector.tensor_scalar(
+            nc.gpsimd.tensor_scalar(
                 out=neg_mean[:],
                 in0=row_sum[:, 0:1],
                 scalar1=row_sum[:, 1:2],
@@ -386,9 +393,24 @@ def tile_successiveswintransfomerblock_pb_kernel(
         def quantise_step(m):
             return max(m - 2, merge_step(min(m + FIRST_ATTN - 1, TILES - 1)))
 
-        for s in range(-1, TILES + 4):
+        for k in range(FIRST_ATTN):
+            attn_transpose(k)
+        spread(0)
+        for k in range(FIRST_ATTN):
+            attn_merge_and_roll(k)
+        spread_copy(0)
+        attn_quantise(0)
+        add_bo2(0)
+
+        for s in range(TILES + 4):
             each(project, s)
+            if s == 0:
+                spread(1)
             each(add_residual, s)
+            if 0 < s + 1 < BO2_ON_VECTOR:
+                add_bo2(s + 1)
+            if s == 1:
+                convert_gain_and_bias()
             each(add_bl, s - 1)
             each(gain_and_bias, s - 3, 0)
             each(square_sum, s - 1)
@@ -397,16 +419,12 @@ def tile_successiveswintransfomerblock_pb_kernel(
             for k in range(TILES):
                 if transpose_step(k) == s:
                     attn_transpose(k)
-            if s == -1:
-                spread(0)
-                spread(1)
             each(linear, s - 4)
             each(scale_and_offset, s - 1)
             for k in range(TILES):
                 if merge_step(k) == s:
                     attn_merge_and_roll(k)
-            if s == -1:
-                spread_copy(0)
+            if s == 0:
                 spread_copy(1)
             each(normalise, s - 1)
             each(h_group, s - 3)
@@ -414,9 +432,7 @@ def tile_successiveswintransfomerblock_pb_kernel(
                 if quantise_step(m) == s:
                     attn_quantise(m)
             each(h_quantise, s - 3)
-            for m in range(TILES):
-                if quantise_step(m) == s:
-                    if m >= BO2_ON_VECTOR:
-                        release_bo2(m)
-                    add_bo2(m)
+            if BO2_ON_VECTOR <= s + 2 < TILES:
+                release_bo2(s + 2)
+                add_bo2(s + 2)
             each(finish, s - 4)

@@ -33,6 +33,8 @@ LN_EPS = 1e-5
 FIRST_ATTN = 3
 BO2_ON_VECTOR = 2
 
+BL_ON_GPSIMD = TILES - 2
+
 FLOPS = 2 * 2 * PATCHES * D * D
 
 
@@ -278,6 +280,13 @@ def tile_successiveswintransfomerblock_pb_kernel(
         def add_bl(m):
             nc.vector.tensor_tensor(out=resid[:, m, :], in0=x_sb[:, m, :], in1=bl_all, op=ADD)
 
+        def add_bl_on_gpsimd(m, half):
+            cols = slice(half * N_BANK, (half + 1) * N_BANK)
+            nc.vector.memset(resid[:, m, half * N_BANK : half * N_BANK + 1], 0.0)
+            nc.gpsimd.tensor_tensor(
+                out=resid[:, m, cols], in0=x_sb[:, m, cols], in1=bl_all[:, cols], op=ADD
+            )
+
         def square_sum(m):
             squares = work.tile([P, D], BF16)
             sq_sum = stats.tile([P, 1], F32)
@@ -411,7 +420,8 @@ def tile_successiveswintransfomerblock_pb_kernel(
                 add_bo2(s + 1)
             if s == 1:
                 convert_gain_and_bias()
-            each(add_bl, s - 1)
+            if s - 1 < BL_ON_GPSIMD:
+                each(add_bl, s - 1)
             each(gain_and_bias, s - 3, 0)
             each(square_sum, s - 1)
             each(gain_and_bias, s - 3, 1)
@@ -435,4 +445,7 @@ def tile_successiveswintransfomerblock_pb_kernel(
             if BO2_ON_VECTOR <= s + 2 < TILES:
                 release_bo2(s + 2)
                 add_bo2(s + 2)
+            for q in range(HALVES * (TILES - BL_ON_GPSIMD)):
+                if TILES - 2 + max(0, q - 1) == s:
+                    add_bl_on_gpsimd(BL_ON_GPSIMD + q // HALVES, q % HALVES)
             each(finish, s - 4)

@@ -441,10 +441,10 @@ def tile_successiveswintransfomerblock_pb_kernel(
             for m in range(TILES):
                 if quantise_step(m) == s:
                     attn_quantise(m)
-            each(h_quantise, s - 3)
             if BO2_ON_VECTOR <= s + 2 < TILES:
                 release_bo2(s + 2)
                 add_bo2(s + 2)
+            each(h_quantise, s - 3)
             for q in range(HALVES * (TILES - BL_ON_GPSIMD)):
                 if TILES - 2 + max(0, q - 1) == s:
                     add_bl_on_gpsimd(BL_ON_GPSIMD + q // HALVES, q % HALVES)

@@ -33,6 +33,7 @@ LN_EPS = 1e-5
 FIRST_ATTN = 3
 BO2_ON_VECTOR = 2
 
+WARM_UP = 4
 BL_ON_GPSIMD = TILES - 2
 
 FLOPS = 2 * 2 * PATCHES * D * D
@@ -73,6 +74,7 @@ def tile_successiveswintransfomerblock_pb_kernel(
         resid = keep.tile([P, TILES, D], F32)
 
         eps = keep.tile([P, 1], F32)
+        idle_rhs = keep.tile([P, N_BANK], BF16)
         warm = keep.tile([P, 1], F32)
         ones = keep.tile([P, P], BF16)
         ident = keep.tile([P, P], F32)
@@ -83,6 +85,7 @@ def tile_successiveswintransfomerblock_pb_kernel(
         gain = keep.tile([P, GROUPS, PACK], F32)
         bias = keep.tile([P, GROUPS, PACK], F32)
 
+        nc.vector.memset(idle_rhs[:].bitcast(I32), 0)
         nc.vector.memset(wo2_planes[:].bitcast(I32), 0)
         nc.vector.memset(eps[:], LN_EPS)
         for which in range(2):
@@ -353,7 +356,8 @@ def tile_successiveswintransfomerblock_pb_kernel(
         def h_group(m):
             h_grouped = work.tile([P, GROUPS, P, PACK], BF16, align_bytes=64)
             nc.vector.tensor_copy(
-                out=h_grouped[:], in_=h_planes_of[m][:].rearrange("p g t n -> p g n t")
+                out=h_grouped[:].rearrange("p g (c i) t -> p g c t i", i=PACK),
+                in_=h_planes_of[m][:].rearrange("p g t (c i) -> p g c t i", i=PACK),
             )
             h_grouped_of[m] = h_grouped
 
@@ -401,6 +405,12 @@ def tile_successiveswintransfomerblock_pb_kernel(
 
         def quantise_step(m):
             return max(m - 2, merge_step(min(m + FIRST_ATTN - 1, TILES - 1)))
+
+        idle_acc = mm_psum.tile([P, N_BANK], F32, tag="mm")
+        for i in range(WARM_UP):
+            nc.tensor.matmul(
+                out=idle_acc[:], lhsT=idle_rhs[:, 0:P], rhs=idle_rhs[:], start=True, stop=True
+            )
 
         for k in range(FIRST_ATTN):
             attn_transpose(k)

@@ -322,8 +322,8 @@ def tile_successiveswintransfomerblock_pb_kernel(
         def normalise(m):
             normed = work.tile([P, D], F32)
             nc.scalar.activation(
-                out=normed[:].rearrange("p (g t q) -> p g q t", g=GROUPS, t=PACK),
-                in_=x_sb[:, m, :].rearrange("p (g q t) -> p g q t", g=GROUPS, t=PACK),
+                out=normed[:],
+                in_=x_sb[:, m, :],
                 func=ACT.Identity,
                 bias=offset_of[m][:],
                 scale=rstd_of[m][:],
@@ -334,9 +334,10 @@ def tile_successiveswintransfomerblock_pb_kernel(
             for g in range(GROUPS):
                 normed_t = tr_psum.tile([P, PACK, P], F32, tag="tr")
                 for t in range(PACK):
-                    block = PACK * g + t
                     nc.tensor.transpose(
-                        normed_t[:, t, :], normed_of[m][:, block * P : (block + 1) * P], ident[:]
+                        normed_t[:, t, :],
+                        normed_of[m][:, K_PASS * g + t : K_PASS * (g + 1) : PACK],
+                        ident[:],
                     )
                 normed_t_of[(m, g)] = normed_t
 

@@ -30,7 +30,15 @@ PATCHES = IMAGES * SIDE * SIDE
 TILES = PATCHES // P
 WINDOWS_PER_TILE = P // (WS * WS)
 LN_EPS = 1e-5
+NV = (8,)
+A_ = slice(0, 512)
+B_ = slice(512, 1024)
+F_ = slice(0, 1024)
+VBO2 = {0: [(1, F_), (2, A_)], 1: [(3, A_), (4, F_)], 2: [(5, A_), (6, F_)], 3: [(7, A_)]}
+VBL = {1: [(0, F_)], 2: [(1, F_)], 3: [(2, A_)], 4: [(2, B_)], 5: [(3, A_)], 6: [(3, B_)], 9: [(8, F_)]}
+GADD = {0: [(1, 2, B_)], 1: [(1, 3, B_)], 2: [(1, 5, B_)], 3: [(1, 7, B_)], 4: [(1, 8, F_)], 5: [(0, 4, F_)], 6: [(0, 5, F_)], 7: [(0, 6, F_)], 8: [(0, 7, A_)], 9: [(0, 7, B_)]}
 FIRST_ATTN = 3
+BO2_SHARED = 5
 BO2_ON_VECTOR = 2
 
 WARM_UP = 4
@@ -85,11 +93,11 @@ def tile_successiveswintransfomerblock_pb_kernel(
         gain = keep.tile([P, GROUPS, PACK], F32)
         bias = keep.tile([P, GROUPS, PACK], F32)
 
+        nc.vector.memset(eps[:], LN_EPS)
+        nc.vector.memset(bias_rows[:, 0, :].bitcast(I32), 0)
         nc.vector.memset(idle_rhs[:].bitcast(I32), 0)
         nc.vector.memset(wo2_planes[:].bitcast(I32), 0)
-        nc.vector.memset(eps[:], LN_EPS)
-        for which in range(2):
-            nc.vector.memset(bias_rows[:, which, :].bitcast(I32), 0)
+        nc.vector.memset(bias_rows[:, 1, :].bitcast(I32), 0)
         nc.vector.memset(ones[:], 1.0)
         nc.vector.memset(wl_planes[:].bitcast(I32), 0)
         make_identity(nc, ident[:])
@@ -118,12 +126,12 @@ def tile_successiveswintransfomerblock_pb_kernel(
         load_rows(xmid_sb, xmid_rows, 0)
         load_words(wo2_w, Wo2_words, 0)
         load_scales(wo2_planes, Wo2_scales)
+        load_rows(attn_sb, attn_rows, FIRST_ATTN)
         load_words(wo2_w, Wo2_words, 1)
-        nc.sync.dma_start(out=bias_rows[0:1, 1, :], in_=bl.unsqueeze(0))
         for m in range(1, TILES):
-            if m + FIRST_ATTN - 1 < TILES:
-                load_rows(attn_sb, attn_rows, m + FIRST_ATTN - 1)
             load_rows(xmid_sb, xmid_rows, m)
+            if m + FIRST_ATTN < TILES:
+                load_rows(attn_sb, attn_rows, m + FIRST_ATTN)
             if m == 1:
                 nc.sync.dma_start(
                     out=gain_bf[:], in_=g4.rearrange("(g p t) -> p g t", g=GROUPS, t=PACK)
@@ -137,6 +145,7 @@ def tile_successiveswintransfomerblock_pb_kernel(
                 load_words(wl_w, Wl_words, 1)
 
         nc.scalar.dma_start(out=bias_rows[0:1, 0, :], in_=bo2.unsqueeze(0))
+        nc.scalar.dma_start(out=bias_rows[0:1, 1, :], in_=bl.unsqueeze(0))
         nc.scalar.activation(out=warm[:], in_=eps[:], func=ACT.Abs_reciprocal_sqrt)
 
         def convert_gain_and_bias():
@@ -159,7 +168,7 @@ def tile_successiveswintransfomerblock_pb_kernel(
         def spread_copy(which):
             for half in range(HALVES):
                 cols = slice(half * N_BANK, (half + 1) * N_BANK)
-                nc.scalar.copy(out=bias_all[:, which, cols], in_=spread_of[(which, half)][:])
+                nc.vector.tensor_copy(out=bias_all[:, which, cols], in_=spread_of[(which, half)][:])
 
         attn_t_of = {}
         acc_of = {}
@@ -220,17 +229,16 @@ def tile_successiveswintransfomerblock_pb_kernel(
                     in_=a_grouped[:, g, places, :].rearrange("p n t -> p (n t)"),
                 )
 
-        def add_bo2(m):
-            engine = nc.vector if m < BO2_ON_VECTOR else nc.gpsimd
+        def add_bo2(m, engine, cols=slice(0, D)):
             engine.tensor_tensor(
-                out=x_sb[:, m, :], in0=xmid_sb[:, m, :], in1=bo2_all, op=ADD
+                out=x_sb[:, m, cols], in0=xmid_sb[:, m, cols], in1=bo2_all[:, cols], op=ADD
             )
 
-        def release_bo2(m):
-            nc.vector.memset(x_sb[:, m, 0:1], 0.0)
+        def release_bo2(m, col=0):
+            nc.vector.memset(x_sb[:, m, col : col + 1], 0.0)
 
-        def product(name, m, lhs_words, lhs_scales, w_words, w_planes):
-            for half in range(HALVES):
+        def product(name, m, lhs_words, lhs_scales, w_words, w_planes, halves=range(HALVES)):
+            for half in halves:
                 cols = slice(half * N_BANK, (half + 1) * N_BANK)
                 acc = mm_psum.tile([P, N_BANK], F32, tag="mm")
                 for g in range(GROUPS):
@@ -245,7 +253,7 @@ def tile_successiveswintransfomerblock_pb_kernel(
                     )
                 acc_of[(name, m, half)] = acc
 
-        def project(m):
+        def project(m, halves=range(HALVES)):
             places = slice(m * P, (m + 1) * P)
             product(
                 "project",
@@ -254,6 +262,7 @@ def tile_successiveswintransfomerblock_pb_kernel(
                 [a_scales[:, g, places] for g in range(GROUPS)],
                 wo2_w,
                 wo2_planes,
+                halves,
             )
 
         def add_residual(m):
@@ -280,8 +289,8 @@ def tile_successiveswintransfomerblock_pb_kernel(
             )
             neg_mean_of[m] = neg_mean
 
-        def add_bl(m):
-            nc.vector.tensor_tensor(out=resid[:, m, :], in0=x_sb[:, m, :], in1=bl_all, op=ADD)
+        def add_bl(m, cols):
+            nc.vector.tensor_tensor(out=resid[:, m, cols], in0=x_sb[:, m, cols], in1=bl_all[:, cols], op=ADD)
 
         def add_bl_on_gpsimd(m, half):
             cols = slice(half * N_BANK, (half + 1) * N_BANK)
@@ -303,7 +312,7 @@ def tile_successiveswintransfomerblock_pb_kernel(
             )
             sq_sum_of[m] = sq_sum
 
-        def scale_and_offset(m):
+        def norm_scale(m):
             rstd = stats.tile([P, 1], F32)
             nc.scalar.activation(
                 out=rstd[:],
@@ -312,15 +321,21 @@ def tile_successiveswintransfomerblock_pb_kernel(
                 bias=eps[:],
                 scale=1.0 / D,
             )
+            rstd_of[m] = rstd
+
+        def norm_offset(m):
             offset = stats.tile([P, 1], F32)
             nc.scalar.activation(
-                out=offset[:], in_=neg_mean_of[m][:], func=ACT.Identity, scale=rstd[:]
+                out=offset[:], in_=neg_mean_of[m][:], func=ACT.Identity, scale=rstd_of[m][:]
             )
-            rstd_of[m] = rstd
             offset_of[m] = offset
 
         def normalise(m):
             normed = work.tile([P, D], F32)
+            if m in NV:
+                nc.vector.tensor_scalar(out=normed[:], in0=x_sb[:, m, :], scalar1=neg_mean_of[m][:], scalar2=rstd_of[m][:], op0=ADD, op1=MULT)
+                normed_of[m] = normed
+                return
             nc.scalar.activation(
                 out=normed[:],
                 in_=x_sb[:, m, :],
@@ -341,11 +356,11 @@ def tile_successiveswintransfomerblock_pb_kernel(
                     )
                 normed_t_of[(m, g)] = normed_t
 
-        def gain_and_bias(m, g):
-            if g == 0:
+        def gain_and_bias(m, g, slots):
+            if (g, slots[0]) == (0, 0):
                 h_planes = work.tile([P, GROUPS, PACK, P], BF16)
                 h_planes_of[m] = h_planes
-            for t in range(PACK):
+            for t in slots:
                 nc.scalar.activation(
                     out=h_planes_of[m][:, g, t, :],
                     in_=normed_t_of[(m, g)][:, t, :],
@@ -413,50 +428,74 @@ def tile_successiveswintransfomerblock_pb_kernel(
                 out=idle_acc[:], lhsT=idle_rhs[:, 0:P], rhs=idle_rhs[:], start=True, stop=True
             )
 
-        for k in range(FIRST_ATTN):
-            attn_transpose(k)
+        attn_transpose(0)
         spread(0)
+        attn_transpose(1)
+        attn_transpose(2)
+        spread(1)
+        spread_copy(0)
         for k in range(FIRST_ATTN):
             attn_merge_and_roll(k)
-        spread_copy(0)
+        add_bo2(0, nc.vector)
         attn_quantise(0)
-        add_bo2(0)
+        spread_copy(1)
 
         for s in range(TILES + 4):
-            each(project, s)
             if s == 0:
-                spread(1)
+                project(0, [0])
+                attn_transpose(FIRST_ATTN)
+                project(0, [1])
+            else:
+                each(project, s)
             each(add_residual, s)
-            if 0 < s + 1 < BO2_ON_VECTOR:
-                add_bo2(s + 1)
+            if s == 0:
+                attn_merge_and_roll(FIRST_ATTN)
+                attn_quantise(1)
+            for m, cols in VBO2.get(s, []):
+                add_bo2(m, nc.vector, cols)
             if s == 1:
                 convert_gain_and_bias()
-            if s - 1 < BL_ON_GPSIMD:
-                each(add_bl, s - 1)
-            each(gain_and_bias, s - 3, 0)
-            each(square_sum, s - 1)
-            each(gain_and_bias, s - 3, 1)
+            for m, cols in VBL.get(s, []):
+                add_bl(m, cols)
+            if s - 1 in NV:
+                each(square_sum, s - 1)
+                each(gain_and_bias, s - 3, 0, range(1))
+                each(norm_scale, s - 1)
+                each(normalise, s - 1)
+                each(gain_and_bias, s - 3, 0, range(1, PACK))
+                each(gain_and_bias, s - 3, 1, range(PACK))
+            else:
+                each(gain_and_bias, s - 3, 0, range(PACK))
+                each(square_sum, s - 1)
+                each(gain_and_bias, s - 3, 1, range(0, 1))
+                each(norm_scale, s - 1)
+                each(gain_and_bias, s - 3, 1, range(1, 2))
+                if s > 2:
+                    each(norm_offset, s - 1)
+                each(gain_and_bias, s - 3, 1, range(2, PACK))
             each(normed_transpose, s - 2)
             for k in range(TILES):
-                if transpose_step(k) == s:
+                if transpose_step(k) == s and k > FIRST_ATTN:
                     attn_transpose(k)
             each(linear, s - 4)
-            each(scale_and_offset, s - 1)
-            for k in range(TILES):
-                if merge_step(k) == s:
-                    attn_merge_and_roll(k)
-            if s == 0:
-                spread_copy(1)
-            each(normalise, s - 1)
+            merges = [k for k in range(FIRST_ATTN + 1, TILES) if merge_step(k) == s]
+            for k in merges[:1]:
+                attn_merge_and_roll(k)
+            if s<=2: each(norm_offset, s - 1)
+            for k in merges[1:]:
+                attn_merge_and_roll(k)
+            if s - 1 not in NV:
+                each(normalise, s - 1)
             each(h_group, s - 3)
             for m in range(TILES):
-                if quantise_step(m) == s:
+                if quantise_step(m) == s and m > 1:
                     attn_quantise(m)
-            if BO2_ON_VECTOR <= s + 2 < TILES:
-                release_bo2(s + 2)
-                add_bo2(s + 2)
+            for kind, m, cols in GADD.get(s, []):
+                t_out = x_sb if kind else resid
+                nc.vector.memset(t_out[:, m, cols.start : cols.start + 1], 0.0)
+                if kind:
+                    add_bo2(m, nc.gpsimd, cols)
+                else:
+                    nc.gpsimd.tensor_tensor(out=resid[:, m, cols], in0=x_sb[:, m, cols], in1=bl_all[:, cols], op=ADD)
             each(h_quantise, s - 3)
-            for q in range(HALVES * (TILES - BL_ON_GPSIMD)):
-                if TILES - 2 + max(0, q - 1) == s:
-                    add_bl_on_gpsimd(BL_ON_GPSIMD + q // HALVES, q % HALVES)
             each(finish, s - 4)

@@ -139,7 +139,7 @@ def tile_successiveswintransfomerblock_pb_kernel(
                 nc.sync.dma_start(
                     out=bias_bf[:], in_=b4.rearrange("(g p t) -> p g t", g=GROUPS, t=PACK)
                 )
-            if m == FIRST_ATTN:
+            if m == 6:
                 load_scales(wl_planes, Wl_scales)
                 load_words(wl_w, Wl_words, 0)
                 load_words(wl_w, Wl_words, 1)

@@ -271,9 +271,9 @@ def tile_successiveswintransfomerblock_pb_kernel(
                 cols = slice(half * N_BANK, (half + 1) * N_BANK)
                 nc.vector.scalar_tensor_tensor(
                     out=x_sb[:, m, cols],
-                    in0=acc_of[("project", m, half)][:],
+                    in0=x_sb[:, m, cols],
                     scalar=1.0,
-                    in1=x_sb[:, m, cols],
+                    in1=acc_of[("project", m, half)][:],
                     op0=MULT,
                     op1=ADD,
                     accum_out=row_sum[:, half : half + 1],
@@ -403,8 +403,8 @@ def tile_successiveswintransfomerblock_pb_kernel(
                 cols = slice(half * N_BANK, (half + 1) * N_BANK)
                 nc.vector.tensor_tensor(
                     out=resid[:, m, cols],
-                    in0=acc_of[("linear", m, half)][:],
-                    in1=resid[:, m, cols],
+                    in0=resid[:, m, cols],
+                    in1=acc_of[("linear", m, half)][:],
                     op=ADD,
                 )
                 nc.sync.dma_start(out=out_rows[m * P : (m + 1) * P, cols], in_=resid[:, m, cols])

@@ -31,12 +31,14 @@ TILES = PATCHES // P
 WINDOWS_PER_TILE = P // (WS * WS)
 LN_EPS = 1e-5
 NV = (8,)
+HS = (8,)
 A_ = slice(0, 512)
 B_ = slice(512, 1024)
 F_ = slice(0, 1024)
-VBO2 = {0: [(1, F_), (2, A_)], 1: [(3, A_), (4, F_)], 2: [(5, A_), (6, F_)], 3: [(7, A_)]}
-VBL = {1: [(0, F_)], 2: [(1, F_)], 3: [(2, A_)], 4: [(2, B_)], 5: [(3, A_)], 6: [(3, B_)], 9: [(8, F_)]}
-GADD = {0: [(1, 2, B_)], 1: [(1, 3, B_)], 2: [(1, 5, B_)], 3: [(1, 7, B_)], 4: [(1, 8, F_)], 5: [(0, 4, F_)], 6: [(0, 5, F_)], 7: [(0, 6, F_)], 8: [(0, 7, A_)], 9: [(0, 7, B_)]}
+XT = {0: [2]}
+VBO2 = {0: [(1, F_)], 1: [(3, A_), (4, F_)], 2: [(5, A_), (6, F_)], 3: [(7, A_)]}
+VBL = {1: [(0, F_)], 2: [(1, F_)], 3: [(2, A_)], 4: [(2, B_)], 5: [(3, A_)], 6: [(3, B_)]}
+GADD = {1: [(1, 3, B_)], 2: [(1, 5, B_)], 3: [(1, 7, B_)], 4: [(1, 8, F_)], 5: [(0, 4, F_)], 6: [(0, 5, F_)], 7: [(0, 6, F_)], 8: [(0, 7, A_)], 9: [(0, 7, B_)], 10: [(0, 8, A_)], 11: [(0, 8, B_)]}
 FIRST_ATTN = 3
 BO2_SHARED = 5
 BO2_ON_VECTOR = 2
@@ -86,6 +88,7 @@ def tile_successiveswintransfomerblock_pb_kernel(
         warm = keep.tile([P, 1], F32)
         ones = keep.tile([P, P], BF16)
         ident = keep.tile([P, P], F32)
+        ident_bf = keep.tile([P, P], BF16)
         bias_rows = keep.tile([P, 2, D], BF16)
         bias_all = keep.tile([P, 2, D], BF16)
         gain_bf = keep.tile([P, GROUPS, PACK], BF16)
@@ -101,6 +104,7 @@ def tile_successiveswintransfomerblock_pb_kernel(
         nc.vector.memset(ones[:], 1.0)
         nc.vector.memset(wl_planes[:].bitcast(I32), 0)
         make_identity(nc, ident[:])
+        make_identity(nc, ident_bf[:])
 
         def load_scales(planes, scales):
             for quad in range(4):
@@ -172,6 +176,7 @@ def tile_successiveswintransfomerblock_pb_kernel(
 
         attn_t_of = {}
         acc_of = {}
+        row_sum_of = {}
         neg_mean_of = {}
         sq_sum_of = {}
         rstd_of = {}
@@ -278,14 +283,17 @@ def tile_successiveswintransfomerblock_pb_kernel(
                     op1=ADD,
                     accum_out=row_sum[:, half : half + 1],
                 )
+            row_sum_of[m] = row_sum
+
+        def minus_mean(m):
+            parts = stats.tile([P, HALVES], F32)
             neg_mean = stats.tile([P, 1], F32)
-            nc.gpsimd.tensor_scalar(
-                out=neg_mean[:],
-                in0=row_sum[:, 0:1],
-                scalar1=row_sum[:, 1:2],
-                scalar2=-1.0 / D,
-                op0=ADD,
-                op1=MULT,
+            nc.scalar.activation(
+                out=parts[:],
+                in_=row_sum_of[m][:],
+                func=ACT.Identity,
+                scale=-1.0 / D,
+                accum_out=neg_mean[:],
             )
             neg_mean_of[m] = neg_mean
 
@@ -371,7 +379,8 @@ def tile_successiveswintransfomerblock_pb_kernel(
 
         def h_group(m):
             h_grouped = work.tile([P, GROUPS, P, PACK], BF16, align_bytes=64)
-            nc.vector.tensor_copy(
+            copy = nc.scalar.copy if m in HS else nc.vector.tensor_copy
+            copy(
                 out=h_grouped[:].rearrange("p g (c i) t -> p g c t i", i=PACK),
                 in_=h_planes_of[m][:].rearrange("p g t (c i) -> p g c t i", i=PACK),
             )
@@ -440,6 +449,19 @@ def tile_successiveswintransfomerblock_pb_kernel(
         attn_quantise(0)
         spread_copy(1)
 
+        def sum_bo2(m):
+            for half in range(HALVES):
+                cols = slice(half * N_BANK, (half + 1) * N_BANK)
+                acc = mm_psum.tile([P, N_BANK], F32, tag="mm")
+                nc.tensor.matmul(out=acc[:], lhsT=ones[:], rhs=bias_rows[:, 0, cols], start=True, stop=False)
+                nc.tensor.matmul(out=acc[:], lhsT=ident_bf[:], rhs=xmid_sb[:, m, cols], start=False, stop=True)
+                acc_of[("bo2", m, half)] = acc
+
+        def copy_sum(m):
+            for half in range(HALVES):
+                cols = slice(half * N_BANK, (half + 1) * N_BANK)
+                nc.scalar.copy(out=x_sb[:, m, cols], in_=acc_of[("bo2", m, half)][:])
+
         for s in range(TILES + 4):
             if s == 0:
                 project(0, [0])
@@ -457,6 +479,7 @@ def tile_successiveswintransfomerblock_pb_kernel(
                 convert_gain_and_bias()
             for m, cols in VBL.get(s, []):
                 add_bl(m, cols)
+            each(minus_mean, s - 1)
             if s - 1 in NV:
                 each(square_sum, s - 1)
                 each(gain_and_bias, s - 3, 0, range(1))
@@ -478,6 +501,8 @@ def tile_successiveswintransfomerblock_pb_kernel(
                 if transpose_step(k) == s and k > FIRST_ATTN:
                     attn_transpose(k)
             each(linear, s - 4)
+            for m in XT.get(s, []):
+                sum_bo2(m)
             merges = [k for k in range(FIRST_ATTN + 1, TILES) if merge_step(k) == s]
             for k in merges[:1]:
                 attn_merge_and_roll(k)
@@ -486,6 +511,8 @@ def tile_successiveswintransfomerblock_pb_kernel(
                 attn_merge_and_roll(k)
             if s - 1 not in NV:
                 each(normalise, s - 1)
+            for m in XT.get(s, []):
+                copy_sum(m)
             each(h_group, s - 3)
             for m in range(TILES):
                 if quantise_step(m) == s and m > 1:

@@ -67,7 +67,7 @@ def tile_successiveswintransfomerblock_pb_kernel(
         stack.enter_context(tc.manual_schedule())
         keep = stack.enter_context(tc.tile_pool(name="keep", bufs=1))
         work = stack.enter_context(tc.tile_pool(name="work", bufs=3))
-        stats = stack.enter_context(tc.tile_pool(name="stats", bufs=4))
+        stats = stack.enter_context(tc.tile_pool(name="stats", bufs=TILES))
         tr_psum = stack.enter_context(tc.psum_pool(name="tr_psum", bufs=4))
         mm_psum = stack.enter_context(tc.psum_pool(name="mm_psum", bufs=4))
 
@@ -97,10 +97,9 @@ def tile_successiveswintransfomerblock_pb_kernel(
         bias = keep.tile([P, GROUPS, PACK], F32)
 
         nc.vector.memset(eps[:], LN_EPS)
-        nc.vector.memset(bias_rows[:, 0, :].bitcast(I32), 0)
         nc.vector.memset(idle_rhs[:].bitcast(I32), 0)
+        nc.vector.memset(bias_rows[:].rearrange("p b d -> p (b d)").bitcast(I32), 0)
         nc.vector.memset(wo2_planes[:].bitcast(I32), 0)
-        nc.vector.memset(bias_rows[:, 1, :].bitcast(I32), 0)
         nc.vector.memset(ones[:], 1.0)
         nc.vector.memset(wl_planes[:].bitcast(I32), 0)
         make_identity(nc, ident[:])
@@ -127,11 +126,14 @@ def tile_successiveswintransfomerblock_pb_kernel(
 
         for m in range(FIRST_ATTN):
             load_rows(attn_sb, attn_rows, m)
+            if m == 1:
+                nc.sync.dma_start(out=bias_rows[0:1, 0, :], in_=bo2.unsqueeze(0))
+                nc.sync.dma_start(out=bias_rows[0:1, 1, :], in_=bl.unsqueeze(0))
         load_rows(xmid_sb, xmid_rows, 0)
         load_words(wo2_w, Wo2_words, 0)
         load_scales(wo2_planes, Wo2_scales)
-        load_rows(attn_sb, attn_rows, FIRST_ATTN)
         load_words(wo2_w, Wo2_words, 1)
+        load_rows(attn_sb, attn_rows, FIRST_ATTN)
         for m in range(1, TILES):
             load_rows(xmid_sb, xmid_rows, m)
             if m + FIRST_ATTN < TILES:
@@ -148,8 +150,6 @@ def tile_successiveswintransfomerblock_pb_kernel(
                 load_words(wl_w, Wl_words, 0)
                 load_words(wl_w, Wl_words, 1)
 
-        nc.scalar.dma_start(out=bias_rows[0:1, 0, :], in_=bo2.unsqueeze(0))
-        nc.scalar.dma_start(out=bias_rows[0:1, 1, :], in_=bl.unsqueeze(0))
         nc.scalar.activation(out=warm[:], in_=eps[:], func=ACT.Abs_reciprocal_sqrt)
 
         def convert_gain_and_bias():
@@ -172,7 +172,8 @@ def tile_successiveswintransfomerblock_pb_kernel(
         def spread_copy(which):
             for half in range(HALVES):
                 cols = slice(half * N_BANK, (half + 1) * N_BANK)
-                nc.vector.tensor_copy(out=bias_all[:, which, cols], in_=spread_of[(which, half)][:])
+                copy = nc.scalar.copy if which else nc.vector.tensor_copy
+                copy(out=bias_all[:, which, cols], in_=spread_of[(which, half)][:])
 
         attn_t_of = {}
         acc_of = {}
@@ -366,7 +367,7 @@ def tile_successiveswintransfomerblock_pb_kernel(
 
         def gain_and_bias(m, g, slots):
             if (g, slots[0]) == (0, 0):
-                h_planes = work.tile([P, GROUPS, PACK, P], BF16)
+                h_planes = stats.tile([P, GROUPS, PACK, P], BF16)
                 h_planes_of[m] = h_planes
             for t in slots:
                 nc.scalar.activation(
@@ -378,7 +379,7 @@ def tile_successiveswintransfomerblock_pb_kernel(
                 )
 
         def h_group(m):
-            h_grouped = work.tile([P, GROUPS, P, PACK], BF16, align_bytes=64)
+            h_grouped = stats.tile([P, GROUPS, P, PACK], BF16, align_bytes=64)
             copy = nc.scalar.copy if m in HS else nc.vector.tensor_copy
             copy(
                 out=h_grouped[:].rearrange("p g (c i) t -> p g c t i", i=PACK),
@@ -387,8 +388,8 @@ def tile_successiveswintransfomerblock_pb_kernel(
             h_grouped_of[m] = h_grouped
 
         def h_quantise(m):
-            h_words = work.tile([P, GROUPS, P], U32, align_bytes=64)
-            h_scales = work.tile([P, GROUPS, P], U8, align_bytes=64)
+            h_words = stats.tile([P, GROUPS, P], U32, align_bytes=64)
+            h_scales = stats.tile([P, GROUPS, P], U8, align_bytes=64)
             nc.vector.quantize_mx(
                 out=h_words[:].rearrange("p g n -> p (g n)").bitcast(FP8X4),
                 scales=h_scales[:].rearrange("p g n -> p (g n)"),
@@ -438,15 +439,16 @@ def tile_successiveswintransfomerblock_pb_kernel(
             )
 
         attn_transpose(0)
-        spread(0)
         attn_transpose(1)
+        spread(0)
         attn_transpose(2)
         spread(1)
         spread_copy(0)
         for k in range(FIRST_ATTN):
             attn_merge_and_roll(k)
-        add_bo2(0, nc.vector)
+        add_bo2(0, nc.vector, A_)
         attn_quantise(0)
+        add_bo2(0, nc.vector, B_)
         spread_copy(1)
 
         def sum_bo2(m):
@@ -463,16 +465,8 @@ def tile_successiveswintransfomerblock_pb_kernel(
                 nc.scalar.copy(out=x_sb[:, m, cols], in_=acc_of[("bo2", m, half)][:])
 
         for s in range(TILES + 4):
-            if s == 0:
-                project(0, [0])
-                attn_transpose(FIRST_ATTN)
-                project(0, [1])
-            else:
-                each(project, s)
+            each(project, s)
             each(add_residual, s)
-            if s == 0:
-                attn_merge_and_roll(FIRST_ATTN)
-                attn_quantise(1)
             for m, cols in VBO2.get(s, []):
                 add_bo2(m, nc.vector, cols)
             if s == 1:
@@ -498,12 +492,12 @@ def tile_successiveswintransfomerblock_pb_kernel(
                 each(gain_and_bias, s - 3, 1, range(2, PACK))
             each(normed_transpose, s - 2)
             for k in range(TILES):
-                if transpose_step(k) == s and k > FIRST_ATTN:
+                if transpose_step(k) == s:
                     attn_transpose(k)
             each(linear, s - 4)
             for m in XT.get(s, []):
                 sum_bo2(m)
-            merges = [k for k in range(FIRST_ATTN + 1, TILES) if merge_step(k) == s]
+            merges = [k for k in range(TILES) if merge_step(k) == s]
             for k in merges[:1]:
                 attn_merge_and_roll(k)
             if s<=2: each(norm_offset, s - 1)
@@ -515,7 +509,7 @@ def tile_successiveswintransfomerblock_pb_kernel(
                 copy_sum(m)
             each(h_group, s - 3)
             for m in range(TILES):
-                if quantise_step(m) == s and m > 1:
+                if quantise_step(m) == s:
                     attn_quantise(m)
             for kind, m, cols in GADD.get(s, []):
                 t_out = x_sb if kind else resid

@@ -30,15 +30,15 @@ PATCHES = IMAGES * SIDE * SIDE
 TILES = PATCHES // P
 WINDOWS_PER_TILE = P // (WS * WS)
 LN_EPS = 1e-5
-NV = (8,)
+NV = (7, 8)
 HS = (8,)
 A_ = slice(0, 512)
 B_ = slice(512, 1024)
 F_ = slice(0, 1024)
-XT = {0: [2]}
+XT = {0: [2], 3: [8]}
 VBO2 = {0: [(1, F_)], 1: [(3, A_), (4, F_)], 2: [(5, A_), (6, F_)], 3: [(7, A_)]}
-VBL = {1: [(0, F_)], 2: [(1, F_)], 3: [(2, A_)], 4: [(2, B_)], 5: [(3, A_)], 6: [(3, B_)]}
-GADD = {1: [(1, 3, B_)], 2: [(1, 5, B_)], 3: [(1, 7, B_)], 4: [(1, 8, F_)], 5: [(0, 4, F_)], 6: [(0, 5, F_)], 7: [(0, 6, F_)], 8: [(0, 7, A_)], 9: [(0, 7, B_)], 10: [(0, 8, A_)], 11: [(0, 8, B_)]}
+VBL = {1: [(0, F_)], 2: [(1, F_)], 3: [(2, A_)], 4: [(2, B_)]}
+GADD = {1: [(1, 3, B_)], 2: [(1, 5, B_)], 3: [(1, 7, B_)], 4: [(0, 3, F_)], 5: [(0, 4, F_)], 6: [(0, 5, F_)], 7: [(0, 6, F_)], 8: [(0, 7, A_)], 9: [(0, 7, B_)], 10: [(0, 8, A_)], 11: [(0, 8, B_)]}
 FIRST_ATTN = 3
 BO2_SHARED = 5
 BO2_ON_VECTOR = 2
@@ -138,7 +138,7 @@ def tile_successiveswintransfomerblock_pb_kernel(
             load_rows(xmid_sb, xmid_rows, m)
             if m + FIRST_ATTN < TILES:
                 load_rows(attn_sb, attn_rows, m + FIRST_ATTN)
-            if m == 1:
+            if m == 3:
                 nc.sync.dma_start(
                     out=gain_bf[:], in_=g4.rearrange("(g p t) -> p g t", g=GROUPS, t=PACK)
                 )
@@ -227,7 +227,7 @@ def tile_successiveswintransfomerblock_pb_kernel(
                         )
 
         def attn_quantise(m):
-            places = slice(m * P, (m + 1) * P)
+            places = slice(m * P, (m + 2) * P if m else P)
             for g in range(GROUPS):
                 nc.vector.quantize_mx(
                     out=a_words[:, g, places].bitcast(FP8X4),
@@ -424,10 +424,10 @@ def tile_successiveswintransfomerblock_pb_kernel(
                 piece(m, *more)
 
         def transpose_step(k):
-            return max(k - 5, (k - FIRST_ATTN) // 2) if k >= FIRST_ATTN else -1
+            return (k - FIRST_ATTN) // 2 if k >= FIRST_ATTN else -1
 
         def merge_step(k):
-            return max(k - 4, transpose_step(k))
+            return transpose_step(k)
 
         def quantise_step(m):
             return max(m - 2, merge_step(min(m + FIRST_ATTN - 1, TILES - 1)))
@@ -490,10 +490,10 @@ def tile_successiveswintransfomerblock_pb_kernel(
                 if s > 2:
                     each(norm_offset, s - 1)
                 each(gain_and_bias, s - 3, 1, range(2, PACK))
-            each(normed_transpose, s - 2)
             for k in range(TILES):
                 if transpose_step(k) == s:
                     attn_transpose(k)
+            each(normed_transpose, s - 2)
             each(linear, s - 4)
             for m in XT.get(s, []):
                 sum_bo2(m)
@@ -508,8 +508,8 @@ def tile_successiveswintransfomerblock_pb_kernel(
             for m in XT.get(s, []):
                 copy_sum(m)
             each(h_group, s - 3)
-            for m in range(TILES):
-                if quantise_step(m) == s:
+            for m in range(1, TILES, 2):
+                if max(m - 2, merge_step(min(m + FIRST_ATTN, TILES - 1))) == s:
                     attn_quantise(m)
             for kind, m, cols in GADD.get(s, []):
                 t_out = x_sb if kind else resid

@@ -35,10 +35,10 @@ HS = (8,)
 A_ = slice(0, 512)
 B_ = slice(512, 1024)
 F_ = slice(0, 1024)
-XT = {0: [2], 3: [8]}
-VBO2 = {0: [(1, F_)], 1: [(3, A_), (4, F_)], 2: [(5, A_), (6, F_)], 3: [(7, A_)]}
-VBL = {1: [(0, F_)], 2: [(1, F_)], 3: [(2, A_)], 4: [(2, B_)]}
-GADD = {1: [(1, 3, B_)], 2: [(1, 5, B_)], 3: [(1, 7, B_)], 4: [(0, 3, F_)], 5: [(0, 4, F_)], 6: [(0, 5, F_)], 7: [(0, 6, F_)], 8: [(0, 7, A_)], 9: [(0, 7, B_)], 10: [(0, 8, A_)], 11: [(0, 8, B_)]}
+XT = {1: [2]}
+VBO2 = {0: [(1, F_)], 1: [(3, A_), (4, A_)], 2: [(5, A_), (6, F_)], 3: [(7, A_)]}
+VBL = {1: [(0, F_)], 2: [(1, F_)], 3: [(2, F_)], 5: [(3, F_)]}
+GADD = {0: [(1, 3, B_)], 1: [(1, 4, B_)], 2: [(1, 5, B_)], 3: [(1, 7, B_)], 4: [(1, 8, F_)], 5: [(0, 4, F_)], 6: [(0, 5, F_)], 7: [(0, 6, F_)], 8: [(0, 7, A_)], 9: [(0, 7, B_)], 10: [(0, 8, A_)], 11: [(0, 8, B_)]}
 FIRST_ATTN = 3
 BO2_SHARED = 5
 BO2_ON_VECTOR = 2
@@ -138,7 +138,7 @@ def tile_successiveswintransfomerblock_pb_kernel(
             load_rows(xmid_sb, xmid_rows, m)
             if m + FIRST_ATTN < TILES:
                 load_rows(attn_sb, attn_rows, m + FIRST_ATTN)
-            if m == 3:
+            if m == 1:
                 nc.sync.dma_start(
                     out=gain_bf[:], in_=g4.rearrange("(g p t) -> p g t", g=GROUPS, t=PACK)
                 )
@@ -227,7 +227,7 @@ def tile_successiveswintransfomerblock_pb_kernel(
                         )
 
         def attn_quantise(m):
-            places = slice(m * P, (m + 2) * P if m else P)
+            places = slice(m * P, (m + (2 if m > 2 else 1)) * P)
             for g in range(GROUPS):
                 nc.vector.quantize_mx(
                     out=a_words[:, g, places].bitcast(FP8X4),
@@ -424,7 +424,7 @@ def tile_successiveswintransfomerblock_pb_kernel(
                 piece(m, *more)
 
         def transpose_step(k):
-            return (k - FIRST_ATTN) // 2 if k >= FIRST_ATTN else -1
+            return (k - FIRST_ATTN) // 2 if k > FIRST_ATTN else -1
 
         def merge_step(k):
             return transpose_step(k)
@@ -465,8 +465,17 @@ def tile_successiveswintransfomerblock_pb_kernel(
                 nc.scalar.copy(out=x_sb[:, m, cols], in_=acc_of[("bo2", m, half)][:])
 
         for s in range(TILES + 4):
-            each(project, s)
+            if s == 0:
+                project(0)
+                attn_transpose(FIRST_ATTN)
+                attn_merge_and_roll(FIRST_ATTN)
+            else:
+                each(project, s)
+            for m in XT.get(s, []):
+                sum_bo2(m)
             each(add_residual, s)
+            if s == 0:
+                attn_quantise(1)
             for m, cols in VBO2.get(s, []):
                 add_bo2(m, nc.vector, cols)
             if s == 1:
@@ -484,6 +493,8 @@ def tile_successiveswintransfomerblock_pb_kernel(
             else:
                 each(gain_and_bias, s - 3, 0, range(PACK))
                 each(square_sum, s - 1)
+                for m in XT.get(s, []):
+                    copy_sum(m)
                 each(gain_and_bias, s - 3, 1, range(0, 1))
                 each(norm_scale, s - 1)
                 each(gain_and_bias, s - 3, 1, range(1, 2))
@@ -495,8 +506,6 @@ def tile_successiveswintransfomerblock_pb_kernel(
                     attn_transpose(k)
             each(normed_transpose, s - 2)
             each(linear, s - 4)
-            for m in XT.get(s, []):
-                sum_bo2(m)
             merges = [k for k in range(TILES) if merge_step(k) == s]
             for k in merges[:1]:
                 attn_merge_and_roll(k)
@@ -505,11 +514,9 @@ def tile_successiveswintransfomerblock_pb_kernel(
                 attn_merge_and_roll(k)
             if s - 1 not in NV:
                 each(normalise, s - 1)
-            for m in XT.get(s, []):
-                copy_sum(m)
             each(h_group, s - 3)
-            for m in range(1, TILES, 2):
-                if max(m - 2, merge_step(min(m + FIRST_ATTN, TILES - 1))) == s:
+            for m in [2, 3, 5, 7]:
+                if max(m - 2, merge_step(min(m + FIRST_ATTN if m > 2 else 4, TILES - 1))) == s:
                     attn_quantise(m)
             for kind, m, cols in GADD.get(s, []):
                 t_out = x_sb if kind else resid

from contextlib import ExitStack

import concourse.mybir as mybir
from concourse.masks import make_identity

FP8X4 = mybir.dt.float8_e4m3fn_x4
BF16 = mybir.dt.bfloat16
F32 = mybir.dt.float32
I32 = mybir.dt.int32
U32 = mybir.dt.uint32
U8 = mybir.dt.uint8
ADD = mybir.AluOpType.add
MULT = mybir.AluOpType.mult
ACT = mybir.ActivationFunctionType

P = 128
PACK = 4
K_PASS = P * PACK
D = 1024
GROUPS = D // K_PASS
N_BANK = 512
HALVES = D // N_BANK
IMAGES = 2
SIDE = 24
WS = 8
SHIFT = WS // 2
WINDOWS_PER_SIDE = SIDE // WS
WINDOWS_PER_IMAGE = WINDOWS_PER_SIDE * WINDOWS_PER_SIDE
PATCHES = IMAGES * SIDE * SIDE
TILES = PATCHES // P
WINDOWS_PER_TILE = P // (WS * WS)
LN_EPS = 1e-5
NV = (7, 8)
HS = (8,)
A_ = slice(0, 512)
B_ = slice(512, 1024)
F_ = slice(0, 1024)
XT = {1: [2]}
VBO2 = {0: [(1, F_)], 1: [(3, A_), (4, A_)], 2: [(5, A_), (6, F_)], 3: [(7, A_)]}
VBL = {1: [(0, F_)], 2: [(1, F_)], 3: [(2, F_)], 5: [(3, F_)]}
GADD = {0: [(1, 3, B_)], 1: [(1, 4, B_)], 2: [(1, 5, B_)], 3: [(1, 7, B_)], 4: [(1, 8, F_)], 5: [(0, 4, F_)], 6: [(0, 5, F_)], 7: [(0, 6, F_)], 8: [(0, 7, A_)], 9: [(0, 7, B_)], 10: [(0, 8, A_)], 11: [(0, 8, B_)]}
FIRST_ATTN = 3
BO2_SHARED = 5
BO2_ON_VECTOR = 2

WARM_UP = 4
BL_ON_GPSIMD = TILES - 2

FLOPS = 2 * 2 * PATCHES * D * D


def rolled_runs(w):
    if w == 0:
        return [(0, SIDE - SHIFT, SHIFT), (SHIFT, 0, SHIFT)]
    return [(0, WS * w - SHIFT, WS)]


def tile_successiveswintransfomerblock_pb_kernel(
    tc, attn_win, x_mid, Wo2_words, Wo2_scales, bo2, g4, b4, Wl_words, Wl_scales, bl, out
):
    nc = tc.nc
    attn_rows = attn_win.flatten_outer_dims()
    xmid_rows = x_mid.flatten_outer_dims()
    out_rows = out.flatten_outer_dims()

    with ExitStack() as stack:
        stack.enter_context(tc.manual_schedule())
        keep = stack.enter_context(tc.tile_pool(name="keep", bufs=1))
        work = stack.enter_context(tc.tile_pool(name="work", bufs=3))
        stats = stack.enter_context(tc.tile_pool(name="stats", bufs=TILES))
        tr_psum = stack.enter_context(tc.psum_pool(name="tr_psum", bufs=4))
        mm_psum = stack.enter_context(tc.psum_pool(name="mm_psum", bufs=4))

        wo2_planes = keep.tile([P, D], U8, align_bytes=64)
        wl_planes = keep.tile([P, D], U8, align_bytes=64)
        wo2_w = keep.tile([P, GROUPS, D], U32, align_bytes=64)
        wl_w = keep.tile([P, GROUPS, D], U32, align_bytes=64)
        attn_sb = keep.tile([P, TILES, D], BF16)
        xmid_sb = keep.tile([P, TILES, D], BF16)
        a_grouped = keep.tile([P, GROUPS, PATCHES, PACK], BF16, align_bytes=64)
        a_words = keep.tile([P, GROUPS, PATCHES], U32, align_bytes=64)
        a_scales = keep.tile([P, GROUPS, PATCHES], U8, align_bytes=64)
        x_sb = keep.tile([P, TILES, D], F32)
        resid = keep.tile([P, TILES, D], F32)

        eps = keep.tile([P, 1], F32)
        idle_rhs = keep.tile([P, N_BANK], BF16)
        warm = keep.tile([P, 1], F32)
        ones = keep.tile([P, P], BF16)
        ident = keep.tile([P, P], F32)
        ident_bf = keep.tile([P, P], BF16)
        bias_rows = keep.tile([P, 2, D], BF16)
        bias_all = keep.tile([P, 2, D], BF16)
        gain_bf = keep.tile([P, GROUPS, PACK], BF16)
        bias_bf = keep.tile([P, GROUPS, PACK], BF16)
        gain = keep.tile([P, GROUPS, PACK], F32)
        bias = keep.tile([P, GROUPS, PACK], F32)

        nc.vector.memset(eps[:], LN_EPS)
        nc.vector.memset(idle_rhs[:].bitcast(I32), 0)
        nc.vector.memset(bias_rows[:].rearrange("p b d -> p (b d)").bitcast(I32), 0)
        nc.vector.memset(wo2_planes[:].bitcast(I32), 0)
        nc.vector.memset(ones[:], 1.0)
        nc.vector.memset(wl_planes[:].bitcast(I32), 0)
        make_identity(nc, ident[:])
        make_identity(nc, ident_bf[:])

        def load_scales(planes, scales):
            for quad in range(4):
                rows = slice(32 * quad, 32 * quad + PACK * GROUPS)
                nc.sync.dma_start(
                    out=planes[rows, :].bitcast(I32),
                    in_=scales[:, 4 * quad : 4 * quad + 4, :].bitcast(I32),
                )

        def load_words(w_tile, words, half):
            nc.sync.dma_start(
                out=w_tile[:, :, half * N_BANK : (half + 1) * N_BANK].bitcast(I32),
                in_=words.rearrange("g p n t -> p g (n t)")[
                    :, :, PACK * half * N_BANK : PACK * (half + 1) * N_BANK
                ].bitcast(I32),
            )

        def load_rows(sb, rows, m):
            nc.sync.dma_start(out=sb[:, m, :], in_=rows[m * P : (m + 1) * P, :])

        for m in range(FIRST_ATTN):
            load_rows(attn_sb, attn_rows, m)
            if m == 1:
                nc.sync.dma_start(out=bias_rows[0:1, 0, :], in_=bo2.unsqueeze(0))
                nc.sync.dma_start(out=bias_rows[0:1, 1, :], in_=bl.unsqueeze(0))
        load_rows(xmid_sb, xmid_rows, 0)
        load_words(wo2_w, Wo2_words, 0)
        load_scales(wo2_planes, Wo2_scales)
        load_words(wo2_w, Wo2_words, 1)
        load_rows(attn_sb, attn_rows, FIRST_ATTN)
        for m in range(1, TILES):
            load_rows(xmid_sb, xmid_rows, m)
            if m + FIRST_ATTN < TILES:
                load_rows(attn_sb, attn_rows, m + FIRST_ATTN)
            if m == 1:
                nc.sync.dma_start(
                    out=gain_bf[:], in_=g4.rearrange("(g p t) -> p g t", g=GROUPS, t=PACK)
                )
                nc.sync.dma_start(
                    out=bias_bf[:], in_=b4.rearrange("(g p t) -> p g t", g=GROUPS, t=PACK)
                )
            if m == 6:
                load_scales(wl_planes, Wl_scales)
                load_words(wl_w, Wl_words, 0)
                load_words(wl_w, Wl_words, 1)

        nc.scalar.activation(out=warm[:], in_=eps[:], func=ACT.Abs_reciprocal_sqrt)

        def convert_gain_and_bias():
            nc.gpsimd.tensor_copy(out=gain[:], in_=gain_bf[:])
            nc.gpsimd.tensor_copy(out=bias[:], in_=bias_bf[:])

        bo2_all = bias_all[:, 0, :]
        bl_all = bias_all[:, 1, :]
        spread_of = {}

        def spread(which):
            for half in range(HALVES):
                cols = slice(half * N_BANK, (half + 1) * N_BANK)
                spread_acc = mm_psum.tile([P, N_BANK], F32, tag="mm")
                nc.tensor.matmul(
                    out=spread_acc[:], lhsT=ones[:], rhs=bias_rows[:, which, cols], start=True, stop=True
                )
                spread_of[(which, half)] = spread_acc

        def spread_copy(which):
            for half in range(HALVES):
                cols = slice(half * N_BANK, (half + 1) * N_BANK)
                copy = nc.scalar.copy if which else nc.vector.tensor_copy
                copy(out=bias_all[:, which, cols], in_=spread_of[(which, half)][:])

        attn_t_of = {}
        acc_of = {}
        row_sum_of = {}
        neg_mean_of = {}
        sq_sum_of = {}
        rstd_of = {}
        offset_of = {}
        normed_of = {}
        normed_t_of = {}
        h_planes_of = {}
        h_grouped_of = {}
        h_words_of = {}
        h_scales_of = {}

        a_pairs = (
            a_grouped[:]
            .rearrange("p g n t -> p (g n t)")
            .bitcast(F32)
            .rearrange("p (g b r c u) -> p g b r c u", g=GROUPS, b=IMAGES, r=SIDE, c=SIDE)
        )

        def attn_transpose(m):
            attn_pairs = attn_sb[:, m, :].bitcast(F32)
            attn_t = tr_psum.tile([P, GROUPS, 2, P], F32, tag="tr")
            for g in range(GROUPS):
                for u in range(2):
                    nc.tensor.transpose(
                        attn_t[:, g, u, :],
                        attn_pairs[:, 2 * P * g + u : 2 * P * (g + 1) : 2],
                        ident[:],
                    )
            attn_t_of[m] = attn_t

        def attn_merge_and_roll(m):
            by_window = attn_t_of[m][:].rearrange(
                "p g u (w i j) -> p g u w i j", w=WINDOWS_PER_TILE, i=WS, j=WS
            )
            for w in range(WINDOWS_PER_TILE):
                window = WINDOWS_PER_TILE * m + w
                b = window // WINDOWS_PER_IMAGE
                wr = (window % WINDOWS_PER_IMAGE) // WINDOWS_PER_SIDE
                wc = window % WINDOWS_PER_SIDE
                for i0, r0, n_rows in rolled_runs(wr):
                    for j0, c0, n_cols in rolled_runs(wc):
                        nc.scalar.copy(
                            out=a_pairs[:, :, b, r0 : r0 + n_rows, c0 : c0 + n_cols, :],
                            in_=by_window[
                                :, :, :, w, i0 : i0 + n_rows, j0 : j0 + n_cols
                            ].rearrange("p g u i j -> p g i j u"),
                        )

        def attn_quantise(m):
            places = slice(m * P, (m + (2 if m > 2 else 1)) * P)
            for g in range(GROUPS):
                nc.vector.quantize_mx(
                    out=a_words[:, g, places].bitcast(FP8X4),
                    scales=a_scales[:, g, places],
                    in_=a_grouped[:, g, places, :].rearrange("p n t -> p (n t)"),
                )

        def add_bo2(m, engine, cols=slice(0, D)):
            engine.tensor_tensor(
                out=x_sb[:, m, cols], in0=xmid_sb[:, m, cols], in1=bo2_all[:, cols], op=ADD
            )

        def release_bo2(m, col=0):
            nc.vector.memset(x_sb[:, m, col : col + 1], 0.0)

        def product(name, m, lhs_words, lhs_scales, w_words, w_planes, halves=range(HALVES)):
            for half in halves:
                cols = slice(half * N_BANK, (half + 1) * N_BANK)
                acc = mm_psum.tile([P, N_BANK], F32, tag="mm")
                for g in range(GROUPS):
                    nc.tensor.matmul_mx(
                        out=acc[:],
                        lhsT=lhs_words[g].bitcast(FP8X4),
                        lhsT_scale=lhs_scales[g],
                        rhs=w_words[:, g, cols].bitcast(FP8X4),
                        rhs_scale=w_planes[PACK * g : P, cols],
                        start=(g == 0),
                        stop=(g == GROUPS - 1),
                    )
                acc_of[(name, m, half)] = acc

        def project(m, halves=range(HALVES)):
            places = slice(m * P, (m + 1) * P)
            product(
                "project",
                m,
                [a_words[:, g, places] for g in range(GROUPS)],
                [a_scales[:, g, places] for g in range(GROUPS)],
                wo2_w,
                wo2_planes,
                halves,
            )

        def add_residual(m):
            row_sum = stats.tile([P, HALVES], F32)
            for half in range(HALVES):
                cols = slice(half * N_BANK, (half + 1) * N_BANK)
                nc.vector.scalar_tensor_tensor(
                    out=x_sb[:, m, cols],
                    in0=x_sb[:, m, cols],
                    scalar=1.0,
                    in1=acc_of[("project", m, half)][:],
                    op0=MULT,
                    op1=ADD,
                    accum_out=row_sum[:, half : half + 1],
                )
            row_sum_of[m] = row_sum

        def minus_mean(m):
            parts = stats.tile([P, HALVES], F32)
            neg_mean = stats.tile([P, 1], F32)
            nc.scalar.activation(
                out=parts[:],
                in_=row_sum_of[m][:],
                func=ACT.Identity,
                scale=-1.0 / D,
                accum_out=neg_mean[:],
            )
            neg_mean_of[m] = neg_mean

        def add_bl(m, cols):
            nc.vector.tensor_tensor(out=resid[:, m, cols], in0=x_sb[:, m, cols], in1=bl_all[:, cols], op=ADD)

        def add_bl_on_gpsimd(m, half):
            cols = slice(half * N_BANK, (half + 1) * N_BANK)
            nc.vector.memset(resid[:, m, half * N_BANK : half * N_BANK + 1], 0.0)
            nc.gpsimd.tensor_tensor(
                out=resid[:, m, cols], in0=x_sb[:, m, cols], in1=bl_all[:, cols], op=ADD
            )

        def square_sum(m):
            squares = work.tile([P, D], BF16)
            sq_sum = stats.tile([P, 1], F32)
            nc.scalar.activation(
                out=squares[:],
                in_=x_sb[:, m, :],
                func=ACT.Square,
                bias=neg_mean_of[m][:],
                scale=1.0,
                accum_out=sq_sum[:],
            )
            sq_sum_of[m] = sq_sum

        def norm_scale(m):
            rstd = stats.tile([P, 1], F32)
            nc.scalar.activation(
                out=rstd[:],
                in_=sq_sum_of[m][:],
                func=ACT.Abs_reciprocal_sqrt,
                bias=eps[:],
                scale=1.0 / D,
            )
            rstd_of[m] = rstd

        def norm_offset(m):
            offset = stats.tile([P, 1], F32)
            nc.scalar.activation(
                out=offset[:], in_=neg_mean_of[m][:], func=ACT.Identity, scale=rstd_of[m][:]
            )
            offset_of[m] = offset

        def normalise(m):
            normed = work.tile([P, D], F32)
            if m in NV:
                nc.vector.tensor_scalar(out=normed[:], in0=x_sb[:, m, :], scalar1=neg_mean_of[m][:], scalar2=rstd_of[m][:], op0=ADD, op1=MULT)
                normed_of[m] = normed
                return
            nc.scalar.activation(
                out=normed[:],
                in_=x_sb[:, m, :],
                func=ACT.Identity,
                bias=offset_of[m][:],
                scale=rstd_of[m][:],
            )
            normed_of[m] = normed

        def normed_transpose(m):
            for g in range(GROUPS):
                normed_t = tr_psum.tile([P, PACK, P], F32, tag="tr")
                for t in range(PACK):
                    nc.tensor.transpose(
                        normed_t[:, t, :],
                        normed_of[m][:, K_PASS * g + t : K_PASS * (g + 1) : PACK],
                        ident[:],
                    )
                normed_t_of[(m, g)] = normed_t

        def gain_and_bias(m, g, slots):
            if (g, slots[0]) == (0, 0):
                h_planes = stats.tile([P, GROUPS, PACK, P], BF16)
                h_planes_of[m] = h_planes
            for t in slots:
                nc.scalar.activation(
                    out=h_planes_of[m][:, g, t, :],
                    in_=normed_t_of[(m, g)][:, t, :],
                    func=ACT.Identity,
                    bias=bias[:, g, t : t + 1],
                    scale=gain[:, g, t : t + 1],
                )

        def h_group(m):
            h_grouped = stats.tile([P, GROUPS, P, PACK], BF16, align_bytes=64)
            copy = nc.scalar.copy if m in HS else nc.vector.tensor_copy
            copy(
                out=h_grouped[:].rearrange("p g (c i) t -> p g c t i", i=PACK),
                in_=h_planes_of[m][:].rearrange("p g t (c i) -> p g c t i", i=PACK),
            )
            h_grouped_of[m] = h_grouped

        def h_quantise(m):
            h_words = stats.tile([P, GROUPS, P], U32, align_bytes=64)
            h_scales = stats.tile([P, GROUPS, P], U8, align_bytes=64)
            nc.vector.quantize_mx(
                out=h_words[:].rearrange("p g n -> p (g n)").bitcast(FP8X4),
                scales=h_scales[:].rearrange("p g n -> p (g n)"),
                in_=h_grouped_of[m][:].rearrange("p g n t -> p (g n t)"),
            )
            h_words_of[m] = h_words
            h_scales_of[m] = h_scales

        def linear(m):
            product(
                "linear",
                m,
                [h_words_of[m][:, g, :] for g in range(GROUPS)],
                [h_scales_of[m][:, g, :] for g in range(GROUPS)],
                wl_w,
                wl_planes,
            )

        def finish(m):
            for half in range(HALVES):
                cols = slice(half * N_BANK, (half + 1) * N_BANK)
                nc.vector.tensor_tensor(
                    out=resid[:, m, cols],
                    in0=resid[:, m, cols],
                    in1=acc_of[("linear", m, half)][:],
                    op=ADD,
                )
                nc.sync.dma_start(out=out_rows[m * P : (m + 1) * P, cols], in_=resid[:, m, cols])

        def each(piece, m, *more):
            if 0 <= m < TILES:
                piece(m, *more)

        def transpose_step(k):
            return (k - FIRST_ATTN) // 2 if k > FIRST_ATTN else -1

        def merge_step(k):
            return transpose_step(k)

        def quantise_step(m):
            return max(m - 2, merge_step(min(m + FIRST_ATTN - 1, TILES - 1)))

        idle_acc = mm_psum.tile([P, N_BANK], F32, tag="mm")
        for i in range(WARM_UP):
            nc.tensor.matmul(
                out=idle_acc[:], lhsT=idle_rhs[:, 0:P], rhs=idle_rhs[:], start=True, stop=True
            )

        attn_transpose(0)
        attn_transpose(1)
        spread(0)
        attn_transpose(2)
        spread(1)
        spread_copy(0)
        for k in range(FIRST_ATTN):
            attn_merge_and_roll(k)
        add_bo2(0, nc.vector, A_)
        attn_quantise(0)
        add_bo2(0, nc.vector, B_)
        spread_copy(1)

        def sum_bo2(m):
            for half in range(HALVES):
                cols = slice(half * N_BANK, (half + 1) * N_BANK)
                acc = mm_psum.tile([P, N_BANK], F32, tag="mm")
                nc.tensor.matmul(out=acc[:], lhsT=ones[:], rhs=bias_rows[:, 0, cols], start=True, stop=False)
                nc.tensor.matmul(out=acc[:], lhsT=ident_bf[:], rhs=xmid_sb[:, m, cols], start=False, stop=True)
                acc_of[("bo2", m, half)] = acc

        def copy_sum(m):
            for half in range(HALVES):
                cols = slice(half * N_BANK, (half + 1) * N_BANK)
                nc.scalar.copy(out=x_sb[:, m, cols], in_=acc_of[("bo2", m, half)][:])

        for s in range(TILES + 4):
            if s == 0:
                project(0)
                attn_transpose(FIRST_ATTN)
                attn_merge_and_roll(FIRST_ATTN)
            else:
                each(project, s)
            for m in XT.get(s, []):
                sum_bo2(m)
            each(add_residual, s)
            if s == 0:
                attn_quantise(1)
            for m, cols in VBO2.get(s, []):
                add_bo2(m, nc.vector, cols)
            if s == 1:
                convert_gain_and_bias()
            for m, cols in VBL.get(s, []):
                add_bl(m, cols)
            each(minus_mean, s - 1)
            if s - 1 in NV:
                each(square_sum, s - 1)
                each(gain_and_bias, s - 3, 0, range(1))
                each(norm_scale, s - 1)
                each(normalise, s - 1)
                each(gain_and_bias, s - 3, 0, range(1, PACK))
                each(gain_and_bias, s - 3, 1, range(PACK))
            else:
                each(gain_and_bias, s - 3, 0, range(PACK))
                each(square_sum, s - 1)
                for m in XT.get(s, []):
                    copy_sum(m)
                each(gain_and_bias, s - 3, 1, range(0, 1))
                each(norm_scale, s - 1)
                each(gain_and_bias, s - 3, 1, range(1, 2))
                if s > 2:
                    each(norm_offset, s - 1)
                each(gain_and_bias, s - 3, 1, range(2, PACK))
            for k in range(TILES):
                if transpose_step(k) == s:
                    attn_transpose(k)
            each(normed_transpose, s - 2)
            each(linear, s - 4)
            merges = [k for k in range(TILES) if merge_step(k) == s]
            for k in merges[:1]:
                attn_merge_and_roll(k)
            if s<=2: each(norm_offset, s - 1)
            for k in merges[1:]:
                attn_merge_and_roll(k)
            if s - 1 not in NV:
                each(normalise, s - 1)
            each(h_group, s - 3)
            for m in [2, 3, 5, 7]:
                if max(m - 2, merge_step(min(m + FIRST_ATTN if m > 2 else 4, TILES - 1))) == s:
                    attn_quantise(m)
            for kind, m, cols in GADD.get(s, []):
                t_out = x_sb if kind else resid
                nc.vector.memset(t_out[:, m, cols.start : cols.start + 1], 0.0)
                if kind:
                    add_bo2(m, nc.gpsimd, cols)
                else:
                    nc.gpsimd.tensor_tensor(out=resid[:, m, cols], in0=x_sb[:, m, cols], in1=bl_all[:, cols], op=ADD)
            each(h_quantise, s - 3)
            each(finish, s - 4)
